import numpy as np
import ml_dtypes


def mxq(x, axis, fmt="e4m3"):
    dtype, down = {"e4m3": (ml_dtypes.float8_e4m3fn, 7), "e5m2": (ml_dtypes.float8_e5m2, 14)}[fmt]
    v = np.moveaxis(np.asarray(x, np.float32).astype(ml_dtypes.bfloat16).astype(np.float64), axis, -1)
    blocks = v.reshape(v.shape[:-1] + (-1, 32))
    amax = np.abs(blocks).max(-1, keepdims=True)
    byte = np.maximum(np.where(amax > 0, np.frexp(amax)[1] - 1 + 127, 0) - down, 1)
    scale = np.exp2(byte - 127.0)
    codes = (blocks / scale).astype(np.float32).astype(dtype).astype(np.float64)
    return np.moveaxis((codes * scale).reshape(v.shape), -1, axis)


WIDE = False


def mx_kscale(k):
    if not WIDE:
        return np.ones(k)
    levels = np.array([10, -10, 5, -5, 0])
    a = np.random.permutation(np.resize(levels, k // 512 * 4)).reshape(k // 512, 4)
    idx = np.arange(k)
    return np.exp2(a[idx // 512, idx % 128 // 32])


BF16 = ml_dtypes.bfloat16


def bf(x):
    return np.asarray(x, np.float32).astype(BF16)


def f64(x):
    return np.asarray(x).astype(np.float64)


E2M1 = np.array([0.0, 0.5, 1.0, 1.5, 2.0, 3.0, 4.0, 6.0, -0.0, -0.5, -1.0, -1.5, -2.0, -3.0, -4.0, -6.0])


def pack_weight(w, fmt):
    k, n = w.shape
    w = f64(bf(w)).reshape(k // 32, 32, n)
    amax = np.abs(w).max(1)
    if fmt == "e4m3":
        byte = np.frexp(amax)[1] - 1 + 127 - 7
    else:
        mant, ex = np.frexp(amax / 6.0)
        byte = np.where(mant > 0.5, ex, ex - 1) + 127
    byte = np.clip(np.where(amax > 0, byte, 1), 1, 254)
    scaled = (w * np.exp2(127.0 - byte)[:, None, :]).reshape(k, n).astype(np.float32)
    by_word = np.ascontiguousarray(scaled.reshape(k // 512, 128, 4, n).transpose(0, 1, 3, 2))
    if fmt == "e4m3":
        words = by_word.astype(ml_dtypes.float8_e4m3fn).view(np.uint8)
    else:
        c = by_word.astype(ml_dtypes.float4_e2m1fn).view(np.uint8) & 0xF
        words = c[..., 0::2] | (c[..., 1::2] << 4)
    return np.ascontiguousarray(words), np.ascontiguousarray(byte.astype(np.uint8).reshape(k // 512, 16, n))


def unpack_weight(words, scales, fmt):
    g, p, n, _ = words.shape
    if fmt == "e4m3":
        vals = np.ascontiguousarray(words).view(ml_dtypes.float8_e4m3fn).astype(np.float64)
    else:
        nib = np.empty((g, p, n, 4), np.uint8)
        nib[..., 0::2] = words & 0xF
        nib[..., 1::2] = words >> 4
        vals = E2M1[nib]
    vals = vals * np.repeat(np.exp2(scales.astype(np.float64) - 127.0), 8, axis=1)[..., None]
    return vals.transpose(0, 1, 3, 2).reshape(g * 512, n)

def pack4(w):
    words, scales = pack_weight(w, "e2m1")
    return words.reshape(words.shape[0], 128, -1), scales


def unpack4(words, scales):
    return unpack_weight(words.reshape(words.shape[0], 128, -1, 2), scales, "e2m1")


B, T, C, H, G = 2, 512, 1024, 16, 16
HS = C // H
TG = T // G
THETA = 10000.0


def apply_rope(t, cos, sin):
    tp = t.reshape(B, T, H, HS // 2, 2)
    a, b = tp[..., 0], tp[..., 1]
    c = cos[None, :, None, :]
    s = sin[None, :, None, :]
    return np.stack([a * c - b * s, a * s + b * c], axis=-1).reshape(B, T, H, HS)


def grp(t):
    return t.reshape(B, G, TG, H, HS).transpose(0, 3, 1, 2, 4)


def with_summary(t):
    return np.concatenate([t, t.mean(axis=3, keepdims=True)], axis=3)


def setup_inputs():
    s = mx_kscale(C)
    x = np.random.standard_normal((B, T, C)) * 0.7 + np.random.standard_normal((B, 1, C)) * 0.7
    w = np.random.standard_normal((3 * C, C)) / np.sqrt(C)
    ang = np.arange(T)[:, None] / THETA ** (np.arange(0, HS, 2) / HS)[None, :]
    words, scales = pack4((w / s[None, :]).T)
    return {"x": bf(x * s), "w_attn_words": words, "w_attn_scales": scales, "freqs_cos": bf(np.cos(ang)), "freqs_sin": bf(np.sin(ang))}


def reference(x, w_attn_words, w_attn_scales, freqs_cos, freqs_sin):
    cos, sin = f64(freqs_cos), f64(freqs_sin)
    qkv = mxq(f64(x), 2, "e4m3") @ unpack4(w_attn_words, w_attn_scales)
    q, k, v = np.split(qkv, 3, axis=2)
    q = apply_rope(q.reshape(B, T, H, HS), cos, sin).reshape(B, T, C)
    k = apply_rope(k.reshape(B, T, H, HS), cos, sin).reshape(B, T, C)
    q, k, v = grp(q), grp(k), grp(v)
    return with_summary(q), with_summary(k), with_summary(v)

@@ -1,0 +1,237 @@
+from contextlib import ExitStack
+
+import concourse.mybir as mybir
+from concourse.masks import make_identity
+
+F32 = mybir.dt.float32
+BF16 = mybir.dt.bfloat16
+I32 = mybir.dt.int32
+U32 = mybir.dt.uint32
+U8 = mybir.dt.uint8
+FP8X4 = mybir.dt.float8_e4m3fn_x4
+FP4X4 = mybir.dt.float4_e2m1fn_x4
+MULT = mybir.AluOpType.mult
+ADD = mybir.AluOpType.add
+
+P = 128
+BATCH, SEQ, CHANNELS = 2, 512, 1024
+HEADS, HEAD = 16, 64
+PAIRS = HEAD // 2
+GROUPS, GROUP = 16, 32
+K_PASS = 4 * P
+PASSES = CHANNELS // K_PASS
+RUN = SEQ // P
+SLOTS = GROUP // RUN
+N_TILE = 512
+TILE_HEADS = N_TILE // HEAD
+WORD_BYTES = 2
+
+FLOPS = 2 * BATCH * SEQ * CHANNELS * 3 * CHANNELS
+
+
+def tile_causalselfattention2_pa_kernel(
+    tc, x, w_attn_words, w_attn_scales, freqs_cos, freqs_sin, out_0, out_1, out_2
+):
+    nc = tc.nc
+    outs = (out_0, out_1, out_2)
+    blocks = [(tensor, half) for half in range(2) for tensor in (1, 0, 2)]
+
+    with ExitStack() as ctx:
+        keep = ctx.enter_context(tc.tile_pool(name="keep", bufs=1))
+        stage = ctx.enter_context(tc.tile_pool(name="stage", bufs=2))
+        cross_pool = ctx.enter_context(tc.tile_pool(name="cross", bufs=6))
+        rows_pool = ctx.enter_context(tc.tile_pool(name="rows", bufs=6))
+        sums_pool = ctx.enter_context(tc.tile_pool(name="sums", bufs=3))
+        acc_pool = ctx.enter_context(tc.psum_pool(name="acc", bufs=6))
+        xt_pool = ctx.enter_context(tc.psum_pool(name="xt", bufs=1))
+        mean_pool = ctx.enter_context(tc.psum_pool(name="mean", bufs=1))
+
+        x_sb = [keep.tile([P, RUN, CHANNELS], BF16, name="x_sb%d" % b) for b in range(BATCH)]
+        x_codes = keep.tile([P, BATCH * RUN, PASSES * P], U32, align_bytes=64)
+        x_scales = keep.tile([P, BATCH * RUN, PASSES * P], U8, align_bytes=64)
+        w_words = keep.tile([P, PASSES, 3 * CHANNELS * WORD_BYTES], U8, align_bytes=64)
+        w_planes = keep.tile([P, PASSES, 3 * CHANNELS], U8, align_bytes=64)
+        cos_bf = keep.tile([P, RUN * PAIRS], BF16)
+        sin_bf = keep.tile([P, RUN * PAIRS], BF16)
+
+        nc.vector.memset(w_planes[:].rearrange("p g n -> p (g n)").bitcast(I32), 0)
+        x_rows = [x[b].rearrange("(p j) k -> p j k", j=RUN) for b in range(BATCH)]
+        nc.sync.dma_start(out=x_sb[0][:, 0, :], in_=x_rows[0][:, 0, :])
+        nc.scalar.dma_start(out=cos_bf[:], in_=freqs_cos.rearrange("(p j) i -> p (j i)", j=RUN))
+        nc.scalar.dma_start(out=sin_bf[:], in_=freqs_sin.rearrange("(p j) i -> p (j i)", j=RUN))
+        for low in range(2):
+            for r in range(4):
+                nc.sync.dma_start(
+                    out=w_planes[32 * low + r : P : 64, :, :].bitcast(I32),
+                    in_=w_attn_scales[:, 4 * low + r : 16 : 8, :]
+                    .rearrange("g q n -> q g n")
+                    .bitcast(I32),
+                )
+
+        def load_w_block(tensor, half):
+            first = (tensor * CHANNELS + half * N_TILE) * WORD_BYTES
+            cols = slice(first, first + N_TILE * WORD_BYTES)
+            nc.sync.dma_start(
+                out=w_words[:, :, cols].bitcast(I32),
+                in_=w_attn_words[:, :, cols].rearrange("g p c -> p g c").bitcast(I32),
+            )
+
+        load_w_block(*blocks[0])
+        for j in range(1, RUN):
+            nc.sync.dma_start(out=x_sb[0][:, j, :], in_=x_rows[0][:, j, :])
+        for block in blocks[1:]:
+            load_w_block(*block)
+        nc.sync.dma_start(out=x_sb[1][:], in_=x_rows[1])
+
+        ident = keep.tile([P, P], F32)
+        make_identity(nc, ident[:])
+        member = keep.tile([P, GROUPS], F32)
+        nc.vector.tensor_reduce(
+            out=member[:],
+            in_=ident[:].rearrange("p (g s) -> p g s", s=SLOTS),
+            axis=mybir.AxisListType.X,
+            op=ADD,
+        )
+        average = keep.tile([P, GROUPS, SLOTS], F32)
+        nc.vector.tensor_scalar_mul(
+            out=average[:],
+            in0=member[:].unsqueeze(2).to_broadcast([P, GROUPS, SLOTS]),
+            scalar1=1.0 / GROUP,
+        )
+        cos_dup = keep.tile([P, RUN, HEAD], F32)
+        nc.vector.tensor_copy(
+            out=cos_dup[:].rearrange("p j (i e) -> p (j i) e", e=2),
+            in_=cos_bf[:].unsqueeze(2).to_broadcast([P, RUN * PAIRS, 2]),
+        )
+        sin_signed = keep.tile([P, RUN, PAIRS, 2], F32)
+        nc.vector.tensor_scalar_mul(
+            out=sin_signed[:, :, :, 0].rearrange("p j i -> p (j i)"), in0=sin_bf[:], scalar1=-1.0
+        )
+        nc.vector.tensor_copy(
+            out=sin_signed[:, :, :, 1].rearrange("p j i -> p (j i)"), in_=sin_bf[:]
+        )
+
+        def quantise_x(b, j):
+            words = x_sb[b][:, j, :].bitcast(F32)
+            xt = xt_pool.tile([P, PASSES, 2, P], F32)
+            for g in range(PASSES):
+                for u in range(2):
+                    nc.tensor.transpose(
+                        xt[:, g, u, :],
+                        words[:, 2 * P * g + u : 2 * P * (g + 1) : 2],
+                        ident[:],
+                    )
+            grouped = stage.tile([P, PASSES * P * 4], BF16, align_bytes=64)
+            nc.scalar.copy(
+                out=grouped[:].bitcast(F32).rearrange("p (g r u) -> p g r u", g=PASSES, u=2),
+                in_=xt[:].rearrange("p g u r -> p g r u"),
+            )
+            nc.vector.quantize_mx(
+                out=x_codes[:, b * RUN + j, :].bitcast(FP8X4),
+                scales=x_scales[:, b * RUN + j, :],
+                in_=grouped[:],
+            )
+
+        def project(b, j, tensor, half):
+            first = tensor * CHANNELS + half * N_TILE
+            acc = acc_pool.tile([P, N_TILE], F32)
+            for g in range(PASSES):
+                tokens = slice(g * P, (g + 1) * P)
+                nc.tensor.matmul_mx(
+                    out=acc[:],
+                    lhsT=x_codes[:, b * RUN + j, tokens].bitcast(FP8X4),
+                    lhsT_scale=x_scales[:, b * RUN + j, tokens],
+                    rhs=w_words[
+                        :, g, first * WORD_BYTES : (first + N_TILE) * WORD_BYTES
+                    ].bitcast(FP4X4),
+                    rhs_scale=w_planes[:, g, first : first + N_TILE],
+                    start=(g == 0),
+                    stop=(g == PASSES - 1),
+                )
+            return acc
+
+        def rope(acc, j, rows):
+            nc.vector.tensor_tensor(
+                out=rows[:, :, j, :],
+                in0=acc[:].rearrange("p (h d) -> p h d", d=HEAD),
+                in1=cos_dup[:, j, :].unsqueeze(1).to_broadcast([P, TILE_HEADS, HEAD]),
+                op=MULT,
+            )
+            pairs = acc[:].rearrange("p (h i e) -> p h i e", i=PAIRS, e=2)
+            cross = cross_pool.tile([P, TILE_HEADS, PAIRS, 2], F32)
+            nc.vector.tensor_tensor(
+                out=cross[:],
+                in0=pairs[:, :, :, ::-1],
+                in1=sin_signed[:, j, :, :].unsqueeze(1).to_broadcast([P, TILE_HEADS, PAIRS, 2]),
+                op=MULT,
+            )
+            nc.gpsimd.tensor_tensor(
+                out=rows[:, :, j, :],
+                in0=rows[:, :, j, :],
+                in1=cross[:].rearrange("p h i e -> p h (i e)"),
+                op=ADD,
+            )
+
+        def block_of_rows(b, tensor, half):
+            rows = rows_pool.tile([P, TILE_HEADS, RUN, HEAD], F32)
+            for j in range(RUN):
+                if b == 0 and (tensor, half) == blocks[0]:
+                    quantise_x(0, j)
+                acc = project(b, j, tensor, half)
+                if tensor < 2:
+                    rope(acc, j, rows)
+                else:
+                    nc.scalar.copy(
+                        out=rows[:, :, j, :], in_=acc[:].rearrange("p (h d) -> p h d", d=HEAD)
+                    )
+            for h in range(TILE_HEADS):
+                nc.sync.dma_start(
+                    out=outs[tensor][b, half * TILE_HEADS + h, :, 0:GROUP, :].rearrange(
+                        "g (s j) d -> g s (j d)", j=RUN
+                    ),
+                    in_=rows[:, h, :, :].rearrange("p j d -> p (j d)"),
+                )
+            return rows
+
+        def group_means(b, tensor, half, rows):
+            sums = sums_pool.tile([P, TILE_HEADS, HEAD], F32)
+            if tensor == 1:
+                first_two = sums_pool.tile([P, TILE_HEADS, HEAD], F32)
+                last_two = sums_pool.tile([P, TILE_HEADS, HEAD], F32)
+                nc.gpsimd.tensor_tensor(
+                    out=first_two[:], in0=rows[:, :, 0, :], in1=rows[:, :, 1, :], op=ADD
+                )
+                nc.gpsimd.tensor_tensor(
+                    out=last_two[:], in0=rows[:, :, 2, :], in1=rows[:, :, 3, :], op=ADD
+                )
+                nc.gpsimd.tensor_tensor(out=sums[:], in0=first_two[:], in1=last_two[:], op=ADD)
+            else:
+                nc.vector.tensor_reduce(
+                    out=sums[:],
+                    in_=rows[:].rearrange("p h j d -> p h d j"),
+                    axis=mybir.AxisListType.X,
+                    op=ADD,
+                )
+            mean_ps = mean_pool.tile([P, N_TILE], F32)
+            nc.tensor.matmul(
+                out=mean_ps[:],
+                lhsT=average[:].rearrange("p g s -> p (g s)"),
+                rhs=sums[:].rearrange("p h d -> p (h d)"),
+                start=True,
+                stop=True,
+            )
+            mean_sb = sums_pool.tile([P, TILE_HEADS, HEAD], F32)
+            nc.scalar.copy(out=mean_sb[:].rearrange("p h d -> p (h d)"), in_=mean_ps[:])
+            heads = slice(half * TILE_HEADS, (half + 1) * TILE_HEADS)
+            nc.sync.dma_start(
+                out=outs[tensor][b, heads, :, GROUP, :].rearrange("h g d -> g h d"),
+                in_=mean_sb[0:P:SLOTS, :, :],
+            )
+
+        for b in range(BATCH):
+            for step, (tensor, half) in enumerate(blocks):
+                rows = block_of_rows(b, tensor, half)
+                group_means(b, tensor, half, rows)
+                if b == 0 and step == 1:
+                    for j in range(RUN):
+                        quantise_x(1, j)

@@ -20,11 +20,14 @@ PAIRS = HEAD // 2
 GROUPS, GROUP = 16, 32
 K_PASS = 4 * P
 PASSES = CHANNELS // K_PASS
-RUN = SEQ // P
+RUN = 8
 SLOTS = GROUP // RUN
+RUNS = SEQ // RUN
 N_TILE = 512
 TILE_HEADS = N_TILE // HEAD
+TURN_HEADS = 4
 WORD_BYTES = 2
+Q, K, V = 0, 1, 2
 
 FLOPS = 2 * BATCH * SEQ * CHANNELS * 3 * CHANNELS
 
@@ -34,70 +37,77 @@ def tile_causalselfattention2_pa_kernel(
 ):
     nc = tc.nc
     outs = (out_0, out_1, out_2)
-    blocks = [(tensor, half) for half in range(2) for tensor in (1, 0, 2)]
+    rope_blocks = [(K, 0), (Q, 0), (K, 1), (Q, 1)]
+    plain_blocks = [(V, 0), (V, 1)]
 
     with ExitStack() as ctx:
         keep = ctx.enter_context(tc.tile_pool(name="keep", bufs=1))
-        stage = ctx.enter_context(tc.tile_pool(name="stage", bufs=2))
-        cross_pool = ctx.enter_context(tc.tile_pool(name="cross", bufs=6))
-        rows_pool = ctx.enter_context(tc.tile_pool(name="rows", bufs=6))
-        sums_pool = ctx.enter_context(tc.tile_pool(name="sums", bufs=3))
-        acc_pool = ctx.enter_context(tc.psum_pool(name="acc", bufs=6))
-        xt_pool = ctx.enter_context(tc.psum_pool(name="xt", bufs=1))
+        stage = ctx.enter_context(tc.tile_pool(name="stage", bufs=3))
+        prod = ctx.enter_context(tc.tile_pool(name="prod", bufs=4))
+        small = ctx.enter_context(tc.tile_pool(name="small", bufs=2))
+        bank_pool = ctx.enter_context(tc.psum_pool(name="bank", bufs=5))
+        turned_pool = ctx.enter_context(tc.psum_pool(name="turned", bufs=2))
         mean_pool = ctx.enter_context(tc.psum_pool(name="mean", bufs=1))
+        ctx.enter_context(tc.manual_schedule())
 
-        x_sb = [keep.tile([P, RUN, CHANNELS], BF16, name="x_sb%d" % b) for b in range(BATCH)]
-        x_codes = keep.tile([P, BATCH * RUN, PASSES * P], U32, align_bytes=64)
-        x_scales = keep.tile([P, BATCH * RUN, PASSES * P], U8, align_bytes=64)
+        x_sb = keep.tile([P, RUN, CHANNELS], BF16)
+        x_codes = keep.tile([P, RUN, PASSES * P], U32, align_bytes=64)
+        x_scales = keep.tile([P, RUN, PASSES * P], U8, align_bytes=64)
         w_words = keep.tile([P, PASSES, 3 * CHANNELS * WORD_BYTES], U8, align_bytes=64)
         w_planes = keep.tile([P, PASSES, 3 * CHANNELS], U8, align_bytes=64)
         cos_bf = keep.tile([P, RUN * PAIRS], BF16)
         sin_bf = keep.tile([P, RUN * PAIRS], BF16)
+        rows = {}
+        for block in rope_blocks + plain_blocks:
+            rows[block] = keep.tile([P, TILE_HEADS, RUN, HEAD], F32, name="rows_%d_%d" % block)
 
         nc.vector.memset(w_planes[:].rearrange("p g n -> p (g n)").bitcast(I32), 0)
-        x_rows = [x[b].rearrange("(p j) k -> p j k", j=RUN) for b in range(BATCH)]
-        nc.sync.dma_start(out=x_sb[0][:, 0, :], in_=x_rows[0][:, 0, :])
-        nc.scalar.dma_start(out=cos_bf[:], in_=freqs_cos.rearrange("(p j) i -> p (j i)", j=RUN))
-        nc.scalar.dma_start(out=sin_bf[:], in_=freqs_sin.rearrange("(p j) i -> p (j i)", j=RUN))
-        for low in range(2):
-            for r in range(4):
-                nc.sync.dma_start(
-                    out=w_planes[32 * low + r : P : 64, :, :].bitcast(I32),
-                    in_=w_attn_scales[:, 4 * low + r : 16 : 8, :]
-                    .rearrange("g q n -> q g n")
-                    .bitcast(I32),
-                )
+        x_tiles = x.rearrange("b (q j) k -> q b j k", j=RUN)
 
-        def load_w_block(tensor, half):
-            first = (tensor * CHANNELS + half * N_TILE) * WORD_BYTES
+        def load_x(j):
+            nc.sync.dma_start(out=x_sb[:, j, :], in_=x_tiles[:, :, j, :])
+
+        def load_w_block(block):
+            first = (block[0] * CHANNELS + block[1] * N_TILE) * WORD_BYTES
             cols = slice(first, first + N_TILE * WORD_BYTES)
             nc.sync.dma_start(
                 out=w_words[:, :, cols].bitcast(I32),
                 in_=w_attn_words[:, :, cols].rearrange("g p c -> p g c").bitcast(I32),
             )
 
-        load_w_block(*blocks[0])
-        for j in range(1, RUN):
-            nc.sync.dma_start(out=x_sb[0][:, j, :], in_=x_rows[0][:, j, :])
-        for block in blocks[1:]:
-            load_w_block(*block)
-        nc.sync.dma_start(out=x_sb[1][:], in_=x_rows[1])
+        def load_table(table_bf, table):
+            nc.scalar.dma_start(
+                out=table_bf[:],
+                in_=table.rearrange("(q j) i -> q (j i)", j=RUN)
+                .unsqueeze(1)
+                .to_broadcast([RUNS, BATCH, RUN * PAIRS]),
+            )
 
+        load_x(0)
+        load_w_block(rope_blocks[0])
+        load_table(cos_bf, freqs_cos)
+        load_table(sin_bf, freqs_sin)
+        for r in range(4):
+            nc.sync.dma_start(
+                out=w_planes[r:P:32, :, :].bitcast(I32),
+                in_=w_attn_scales[:, r:16:4, :].rearrange("g q n -> q g n").bitcast(I32),
+            )
+        load_x(1)
+        load_x(2)
+        load_w_block(plain_blocks[0])
+        for j in range(3, RUN):
+            load_x(j)
+        for block in (rope_blocks[1], plain_blocks[1], rope_blocks[2], rope_blocks[3]):
+            load_w_block(block)
+
+        warm = keep.tile([P, 2], F32)
+        nc.vector.memset(warm[:, 0:1], 0.0)
+        nc.scalar.copy(out=warm[:, 1:2], in_=warm[:, 0:1])
         ident = keep.tile([P, P], F32)
         make_identity(nc, ident[:])
-        member = keep.tile([P, GROUPS], F32)
-        nc.vector.tensor_reduce(
-            out=member[:],
-            in_=ident[:].rearrange("p (g s) -> p g s", s=SLOTS),
-            axis=mybir.AxisListType.X,
-            op=ADD,
-        )
-        average = keep.tile([P, GROUPS, SLOTS], F32)
-        nc.vector.tensor_scalar_mul(
-            out=average[:],
-            in0=member[:].unsqueeze(2).to_broadcast([P, GROUPS, SLOTS]),
-            scalar1=1.0 / GROUP,
-        )
+        fold = keep.tile([P, HEAD], F32)
+        nc.vector.tensor_tensor(out=fold[:], in0=ident[:, 0:HEAD], in1=ident[:, HEAD:P], op=ADD)
+        nc.vector.tensor_scalar_mul(out=fold[:], in0=fold[:], scalar1=1.0 / GROUP)
         cos_dup = keep.tile([P, RUN, HEAD], F32)
         nc.vector.tensor_copy(
             out=cos_dup[:].rearrange("p j (i e) -> p (j i) e", e=2),
@@ -111,9 +121,9 @@ def tile_causalselfattention2_pa_kernel(
             out=sin_signed[:, :, :, 1].rearrange("p j i -> p (j i)"), in_=sin_bf[:]
         )
 
-        def quantise_x(b, j):
-            words = x_sb[b][:, j, :].bitcast(F32)
-            xt = xt_pool.tile([P, PASSES, 2, P], F32)
+        def prepare_x(j):
+            words = x_sb[:, j, :].bitcast(F32)
+            xt = bank_pool.tile([P, PASSES, 2, P], F32, tag="bank")
             for g in range(PASSES):
                 for u in range(2):
                     nc.tensor.transpose(
@@ -127,20 +137,20 @@ def tile_causalselfattention2_pa_kernel(
                 in_=xt[:].rearrange("p g u r -> p g r u"),
             )
             nc.vector.quantize_mx(
-                out=x_codes[:, b * RUN + j, :].bitcast(FP8X4),
-                scales=x_scales[:, b * RUN + j, :],
+                out=x_codes[:, j, :].bitcast(FP8X4),
+                scales=x_scales[:, j, :],
                 in_=grouped[:],
             )
 
-        def project(b, j, tensor, half):
-            first = tensor * CHANNELS + half * N_TILE
-            acc = acc_pool.tile([P, N_TILE], F32)
+        def project(j, block):
+            first = block[0] * CHANNELS + block[1] * N_TILE
+            acc = bank_pool.tile([P, N_TILE], F32, tag="bank")
             for g in range(PASSES):
                 tokens = slice(g * P, (g + 1) * P)
                 nc.tensor.matmul_mx(
                     out=acc[:],
-                    lhsT=x_codes[:, b * RUN + j, tokens].bitcast(FP8X4),
-                    lhsT_scale=x_scales[:, b * RUN + j, tokens],
+                    lhsT=x_codes[:, j, tokens].bitcast(FP8X4),
+                    lhsT_scale=x_scales[:, j, tokens],
                     rhs=w_words[
                         :, g, first * WORD_BYTES : (first + N_TILE) * WORD_BYTES
                     ].bitcast(FP4X4),
@@ -150,88 +160,147 @@ def tile_causalselfattention2_pa_kernel(
                 )
             return acc
 
-        def rope(acc, j, rows):
+        def rope_products(acc, j):
+            direct = prod.tile([P, TILE_HEADS, HEAD], F32)
             nc.vector.tensor_tensor(
-                out=rows[:, :, j, :],
+                out=direct[:],
                 in0=acc[:].rearrange("p (h d) -> p h d", d=HEAD),
                 in1=cos_dup[:, j, :].unsqueeze(1).to_broadcast([P, TILE_HEADS, HEAD]),
                 op=MULT,
             )
             pairs = acc[:].rearrange("p (h i e) -> p h i e", i=PAIRS, e=2)
-            cross = cross_pool.tile([P, TILE_HEADS, PAIRS, 2], F32)
+            cross = prod.tile([P, TILE_HEADS, PAIRS, 2], F32)
             nc.vector.tensor_tensor(
                 out=cross[:],
                 in0=pairs[:, :, :, ::-1],
                 in1=sin_signed[:, j, :, :].unsqueeze(1).to_broadcast([P, TILE_HEADS, PAIRS, 2]),
                 op=MULT,
             )
+            return direct, cross
+
+        def rope_sum(block, j, direct, cross):
             nc.gpsimd.tensor_tensor(
-                out=rows[:, :, j, :],
-                in0=rows[:, :, j, :],
+                out=rows[block][:, :, j, :],
+                in0=direct[:],
                 in1=cross[:].rearrange("p h i e -> p h (i e)"),
                 op=ADD,
             )
 
-        def block_of_rows(b, tensor, half):
-            rows = rows_pool.tile([P, TILE_HEADS, RUN, HEAD], F32)
-            for j in range(RUN):
-                if b == 0 and (tensor, half) == blocks[0]:
-                    quantise_x(0, j)
-                acc = project(b, j, tensor, half)
-                if tensor < 2:
-                    rope(acc, j, rows)
-                else:
-                    nc.scalar.copy(
-                        out=rows[:, :, j, :], in_=acc[:].rearrange("p (h d) -> p h d", d=HEAD)
-                    )
-            for h in range(TILE_HEADS):
-                nc.sync.dma_start(
-                    out=outs[tensor][b, half * TILE_HEADS + h, :, 0:GROUP, :].rearrange(
-                        "g (s j) d -> g s (j d)", j=RUN
-                    ),
-                    in_=rows[:, h, :, :].rearrange("p j d -> p (j d)"),
-                )
-            return rows
+        def plain_bank(j, block):
+            acc = project(j, block)
+            nc.scalar.copy(
+                out=rows[block][:, :, j, :], in_=acc[:].rearrange("p (h d) -> p h d", d=HEAD)
+            )
 
-        def group_means(b, tensor, half, rows):
-            sums = sums_pool.tile([P, TILE_HEADS, HEAD], F32)
-            if tensor == 1:
-                first_two = sums_pool.tile([P, TILE_HEADS, HEAD], F32)
-                last_two = sums_pool.tile([P, TILE_HEADS, HEAD], F32)
-                nc.gpsimd.tensor_tensor(
-                    out=first_two[:], in0=rows[:, :, 0, :], in1=rows[:, :, 1, :], op=ADD
-                )
-                nc.gpsimd.tensor_tensor(
-                    out=last_two[:], in0=rows[:, :, 2, :], in1=rows[:, :, 3, :], op=ADD
-                )
-                nc.gpsimd.tensor_tensor(out=sums[:], in0=first_two[:], in1=last_two[:], op=ADD)
-            else:
-                nc.vector.tensor_reduce(
-                    out=sums[:],
-                    in_=rows[:].rearrange("p h j d -> p h d j"),
-                    axis=mybir.AxisListType.X,
-                    op=ADD,
-                )
-            mean_ps = mean_pool.tile([P, N_TILE], F32)
+        def store_rows(block):
+            for h in range(TILE_HEADS):
+                for b in range(BATCH):
+                    nc.sync.dma_start(
+                        out=outs[block[0]][
+                            b, block[1] * TILE_HEADS + h, :, 0:GROUP, :
+                        ].rearrange("g (s j) d -> g s (j d)", j=RUN),
+                        in_=rows[block][b:P:2, h, :, :].rearrange("p j d -> p (j d)"),
+                    )
+
+        def turn_sums(block, part):
+            turned = turned_pool.tile([P, TURN_HEADS, P], F32)
+            for hh in range(TURN_HEADS):
+                for m in range(RUN // 2):
+                    nc.tensor.matmul(
+                        out=turned[:, hh, :],
+                        lhsT=rows[block][
+                            :, part * TURN_HEADS + hh, 2 * m : 2 * m + 2, :
+                        ].rearrange("p j d -> p (j d)"),
+                        rhs=ident[:],
+                        is_transpose=True,
+                        start=(m == 0),
+                        stop=(m == RUN // 2 - 1),
+                    )
+            return turned
+
+        def reduce_slots(turned):
+            sums = small.tile([P, TURN_HEADS * GROUPS, BATCH], F32)
+            nc.vector.tensor_reduce(
+                out=sums[:],
+                in_=turned[:].rearrange("p h (g s b) -> p (h g) b s", s=SLOTS, b=BATCH),
+                axis=mybir.AxisListType.X,
+                op=ADD,
+            )
+            return sums
+
+        def fold_and_store(block, part, sums):
+            mean_ps = mean_pool.tile([P, HEAD], F32)
             nc.tensor.matmul(
                 out=mean_ps[:],
-                lhsT=average[:].rearrange("p g s -> p (g s)"),
-                rhs=sums[:].rearrange("p h d -> p (h d)"),
+                lhsT=sums[:].rearrange("p q b -> p (q b)"),
+                rhs=fold[:],
                 start=True,
                 stop=True,
             )
-            mean_sb = sums_pool.tile([P, TILE_HEADS, HEAD], F32)
-            nc.scalar.copy(out=mean_sb[:].rearrange("p h d -> p (h d)"), in_=mean_ps[:])
-            heads = slice(half * TILE_HEADS, (half + 1) * TILE_HEADS)
-            nc.sync.dma_start(
-                out=outs[tensor][b, heads, :, GROUP, :].rearrange("h g d -> g h d"),
-                in_=mean_sb[0:P:SLOTS, :, :],
+            mean_sb = small.tile([P, HEAD], F32)
+            nc.scalar.copy(out=mean_sb[:], in_=mean_ps[:])
+            first = (block[1] * TILE_HEADS + part * TURN_HEADS) * GROUPS
+            nc.scalar.dma_start(
+                out=outs[block[0]]
+                .rearrange("b h g r d -> b (h g) r d")[
+                    :, first : first + TURN_HEADS * GROUPS, GROUP, :
+                ]
+                .rearrange("b q d -> q b d"),
+                in_=mean_sb[:],
             )
 
-        for b in range(BATCH):
-            for step, (tensor, half) in enumerate(blocks):
-                rows = block_of_rows(b, tensor, half)
-                group_means(b, tensor, half, rows)
-                if b == 0 and step == 1:
-                    for j in range(RUN):
-                        quantise_x(1, j)
+        AHEAD = 3
+        for j in range(AHEAD):
+            prepare_x(j)
+
+        steps = [(block, j) for block in rope_blocks for j in range(RUN)]
+        jobs = []
+        to_reduce = []
+        to_fold = []
+        for n, (block, j) in enumerate(steps):
+            acc = project(j, block)
+            direct, cross = rope_products(acc, j)
+            if to_reduce:
+                job_block, job_part, turned = to_reduce[0]
+                to_reduce = to_reduce[1:]
+                to_fold.append((job_block, job_part, reduce_slots(turned)))
+            rope_sum(block, j, direct, cross)
+            done = []
+            if n < RUN:
+                plain_bank(j, plain_blocks[0])
+                if j == RUN - 1:
+                    done.append(plain_blocks[0])
+                if j + AHEAD < RUN:
+                    prepare_x(j + AHEAD)
+            elif n < 3 * RUN and n % 2 == 0:
+                plain_bank((n - RUN) // 2, plain_blocks[1])
+                if (n - RUN) // 2 == RUN - 1:
+                    done.append(plain_blocks[1])
+            if j == RUN - 1:
+                done.append(block)
+            for finished in done:
+                store_rows(finished)
+                for part in range(TILE_HEADS // TURN_HEADS):
+                    jobs.append((finished, part, n + 2))
+            if n % 2 == 1:
+                if to_fold:
+                    fold_and_store(*to_fold[0])
+                    to_fold = to_fold[1:]
+                if jobs and jobs[0][2] <= n:
+                    job_block, job_part, ready = jobs[0]
+                    jobs = jobs[1:]
+                    to_reduce.append((job_block, job_part, turn_sums(job_block, job_part)))
+
+        for job_block, job_part, ready in jobs:
+            to_reduce.append((job_block, job_part, turn_sums(job_block, job_part)))
+            if len(to_reduce) > 1:
+                first_block, first_part, turned = to_reduce[0]
+                to_reduce = to_reduce[1:]
+                to_fold.append((first_block, first_part, reduce_slots(turned)))
+            if to_fold:
+                fold_and_store(*to_fold[0])
+                to_fold = to_fold[1:]
+        for job_block, job_part, turned in to_reduce:
+            to_fold.append((job_block, job_part, reduce_slots(turned)))
+        for waiting in to_fold:
+            fold_and_store(*waiting)

@@ -26,6 +26,9 @@ RUNS = SEQ // RUN
 N_TILE = 512
 TILE_HEADS = N_TILE // HEAD
 TURN_HEADS = 4
+PAIR_HEADS = 2
+N_PAIR = PAIR_HEADS * HEAD
+PAIR_RUN = N_TILE // N_PAIR
 WORD_BYTES = 2
 Q, K, V = 0, 1, 2
 
@@ -53,13 +56,17 @@ def tile_causalselfattention2_pa_kernel(
         x_sb = keep.tile([P, RUN, CHANNELS], BF16)
         x_codes = keep.tile([P, RUN, PASSES * P], U32, align_bytes=64)
         x_scales = keep.tile([P, RUN, PASSES * P], U8, align_bytes=64)
-        w_words = keep.tile([P, PASSES, 3 * CHANNELS * WORD_BYTES], U8, align_bytes=64)
         w_planes = keep.tile([P, PASSES, 3 * CHANNELS], U8, align_bytes=64)
         cos_bf = keep.tile([P, RUN * PAIRS], BF16)
         sin_bf = keep.tile([P, RUN * PAIRS], BF16)
+        means = keep.tile([P, 3 * HEADS // TURN_HEADS, HEAD], F32)
         rows = {}
+        w_words = {}
         for block in rope_blocks + plain_blocks:
             rows[block] = keep.tile([P, TILE_HEADS, RUN, HEAD], F32, name="rows_%d_%d" % block)
+            w_words[block] = keep.tile(
+                [P, PASSES, N_TILE * WORD_BYTES], U8, name="w_words_%d_%d" % block, align_bytes=64
+            )
 
         nc.vector.memset(w_planes[:].rearrange("p g n -> p (g n)").bitcast(I32), 0)
         x_tiles = x.rearrange("b (q j) k -> q b j k", j=RUN)
@@ -71,31 +78,34 @@ def tile_causalselfattention2_pa_kernel(
             first = (block[0] * CHANNELS + block[1] * N_TILE) * WORD_BYTES
             cols = slice(first, first + N_TILE * WORD_BYTES)
             nc.sync.dma_start(
-                out=w_words[:, :, cols].bitcast(I32),
+                out=w_words[block][:].bitcast(I32),
                 in_=w_attn_words[:, :, cols].rearrange("g p c -> p g c").bitcast(I32),
             )
 
-        def load_table(table_bf, table):
-            nc.scalar.dma_start(
+        def load_table(queue, table_bf, table):
+            queue.dma_start(
                 out=table_bf[:],
                 in_=table.rearrange("(q j) i -> q (j i)", j=RUN)
                 .unsqueeze(1)
                 .to_broadcast([RUNS, BATCH, RUN * PAIRS]),
             )
 
+        ident = keep.tile([P, P], F32)
+        make_identity(nc, ident[:])
         load_x(0)
+        load_x(1)
         load_w_block(rope_blocks[0])
-        load_table(cos_bf, freqs_cos)
-        load_table(sin_bf, freqs_sin)
         for r in range(4):
             nc.sync.dma_start(
                 out=w_planes[r:P:32, :, :].bitcast(I32),
                 in_=w_attn_scales[:, r:16:4, :].rearrange("g q n -> q g n").bitcast(I32),
             )
-        load_x(1)
+        load_table(nc.scalar, cos_bf, freqs_cos)
+        load_table(nc.sync, sin_bf, freqs_sin)
         load_x(2)
+        load_x(3)
         load_w_block(plain_blocks[0])
-        for j in range(3, RUN):
+        for j in range(4, RUN):
             load_x(j)
         for block in (rope_blocks[1], plain_blocks[1], rope_blocks[2], rope_blocks[3]):
             load_w_block(block)
@@ -103,8 +113,6 @@ def tile_causalselfattention2_pa_kernel(
         warm = keep.tile([P, 2], F32)
         nc.vector.memset(warm[:, 0:1], 0.0)
         nc.scalar.copy(out=warm[:, 1:2], in_=warm[:, 0:1])
-        ident = keep.tile([P, P], F32)
-        make_identity(nc, ident[:])
         fold = keep.tile([P, HEAD], F32)
         nc.vector.tensor_tensor(out=fold[:], in0=ident[:, 0:HEAD], in1=ident[:, HEAD:P], op=ADD)
         nc.vector.tensor_scalar_mul(out=fold[:], in0=fold[:], scalar1=1.0 / GROUP)
@@ -114,12 +122,14 @@ def tile_causalselfattention2_pa_kernel(
             in_=cos_bf[:].unsqueeze(2).to_broadcast([P, RUN * PAIRS, 2]),
         )
         sin_signed = keep.tile([P, RUN, PAIRS, 2], F32)
-        nc.vector.tensor_scalar_mul(
-            out=sin_signed[:, :, :, 0].rearrange("p j i -> p (j i)"), in0=sin_bf[:], scalar1=-1.0
-        )
-        nc.vector.tensor_copy(
-            out=sin_signed[:, :, :, 1].rearrange("p j i -> p (j i)"), in_=sin_bf[:]
-        )
+
+        def widen_sin():
+            nc.vector.tensor_scalar_mul(
+                out=sin_signed[:, :, :, 0].rearrange("p j i -> p (j i)"), in0=sin_bf[:], scalar1=-1.0
+            )
+            nc.vector.tensor_copy(
+                out=sin_signed[:, :, :, 1].rearrange("p j i -> p (j i)"), in_=sin_bf[:]
+            )
 
         def prepare_x(j):
             words = x_sb[:, j, :].bitcast(F32)
@@ -151,25 +161,75 @@ def tile_causalselfattention2_pa_kernel(
                     out=acc[:],
                     lhsT=x_codes[:, j, tokens].bitcast(FP8X4),
                     lhsT_scale=x_scales[:, j, tokens],
-                    rhs=w_words[
-                        :, g, first * WORD_BYTES : (first + N_TILE) * WORD_BYTES
-                    ].bitcast(FP4X4),
+                    rhs=w_words[block][:, g, :].bitcast(FP4X4),
                     rhs_scale=w_planes[:, g, first : first + N_TILE],
                     start=(g == 0),
                     stop=(g == PASSES - 1),
                 )
             return acc
 
-        def rope_products(acc, j):
-            direct = prod.tile([P, TILE_HEADS, HEAD], F32)
+        def project_pair(first_j, block, pair):
+            first = block[0] * CHANNELS + block[1] * N_TILE + pair * N_PAIR
+            acc = bank_pool.tile([P, PAIR_RUN, N_PAIR], F32, tag="bank")
+            for jj in range(PAIR_RUN):
+                for g in range(PASSES):
+                    tokens = slice(g * P, (g + 1) * P)
+                    nc.tensor.matmul_mx(
+                        out=acc[:, jj, :],
+                        lhsT=x_codes[:, first_j + jj, tokens].bitcast(FP8X4),
+                        lhsT_scale=x_scales[:, first_j + jj, tokens],
+                        rhs=w_words[block][
+                            :, g, pair * N_PAIR * WORD_BYTES : (pair + 1) * N_PAIR * WORD_BYTES
+                        ].bitcast(FP4X4),
+                        rhs_scale=w_planes[:, g, first : first + N_PAIR],
+                        start=(g == 0),
+                        stop=(g == PASSES - 1),
+                    )
+            return acc
+
+        def rope_products_pair(acc, first_j):
+            some = slice(first_j, first_j + PAIR_RUN)
+            direct = prod.tile([P, PAIR_RUN, PAIR_HEADS, HEAD], F32, tag="direct")
+            nc.vector.tensor_tensor(
+                out=direct[:],
+                in0=acc[:].rearrange("p j (h d) -> p j h d", d=HEAD),
+                in1=cos_dup[:, some, :].unsqueeze(2).to_broadcast([P, PAIR_RUN, PAIR_HEADS, HEAD]),
+                op=MULT,
+            )
+            pairs = acc[:].rearrange("p j (h i e) -> p j h i e", i=PAIRS, e=2)
+            cross = prod.tile([P, PAIR_RUN, PAIR_HEADS, PAIRS, 2], F32, tag="cross")
+            nc.vector.tensor_tensor(
+                out=cross[:],
+                in0=pairs[:, :, :, :, ::-1],
+                in1=sin_signed[:, some, :, :]
+                .unsqueeze(2)
+                .to_broadcast([P, PAIR_RUN, PAIR_HEADS, PAIRS, 2]),
+                op=MULT,
+            )
+            return direct, cross
+
+        def rope_sum_pair(block, pair, first_j, direct, cross):
+            nc.gpsimd.tensor_tensor(
+                out=rows[block][
+                    :, pair * PAIR_HEADS : (pair + 1) * PAIR_HEADS, first_j : first_j + PAIR_RUN, :
+                ].rearrange("p h j d -> p j h d"),
+                in0=direct[:],
+                in1=cross[:].rearrange("p j h i e -> p j h (i e)"),
+                op=ADD,
+            )
+
+        def rope_products(acc, j, first):
+            direct = prod.tile([P, TILE_HEADS, HEAD], F32, tag="direct")
             nc.vector.tensor_tensor(
                 out=direct[:],
                 in0=acc[:].rearrange("p (h d) -> p h d", d=HEAD),
                 in1=cos_dup[:, j, :].unsqueeze(1).to_broadcast([P, TILE_HEADS, HEAD]),
                 op=MULT,
             )
+            if first:
+                widen_sin()
             pairs = acc[:].rearrange("p (h i e) -> p h i e", i=PAIRS, e=2)
-            cross = prod.tile([P, TILE_HEADS, PAIRS, 2], F32)
+            cross = prod.tile([P, TILE_HEADS, PAIRS, 2], F32, tag="cross")
             nc.vector.tensor_tensor(
                 out=cross[:],
                 in0=pairs[:, :, :, ::-1],
@@ -192,8 +252,8 @@ def tile_causalselfattention2_pa_kernel(
                 out=rows[block][:, :, j, :], in_=acc[:].rearrange("p (h d) -> p h d", d=HEAD)
             )
 
-        def store_rows(block):
-            for h in range(TILE_HEADS):
+        def store_rows(block, heads):
+            for h in heads:
                 for b in range(BATCH):
                     nc.sync.dma_start(
                         out=outs[block[0]][
@@ -237,70 +297,74 @@ def tile_causalselfattention2_pa_kernel(
                 start=True,
                 stop=True,
             )
-            mean_sb = small.tile([P, HEAD], F32)
-            nc.scalar.copy(out=mean_sb[:], in_=mean_ps[:])
+            mean_sb = means[:, 4 * block[0] + 2 * block[1] + part, :]
+            nc.scalar.copy(out=mean_sb, in_=mean_ps[:])
             first = (block[1] * TILE_HEADS + part * TURN_HEADS) * GROUPS
-            nc.scalar.dma_start(
+            nc.sync.dma_start(
                 out=outs[block[0]]
                 .rearrange("b h g r d -> b (h g) r d")[
                     :, first : first + TURN_HEADS * GROUPS, GROUP, :
                 ]
                 .rearrange("b q d -> q b d"),
-                in_=mean_sb[:],
+                in_=mean_sb,
             )
 
-        AHEAD = 3
+        AHEAD = 2
+        PLAIN_LAG = 2
+        FIRST_TURN = RUN + 1
+        PARTS = TILE_HEADS // TURN_HEADS
         for j in range(AHEAD):
             prepare_x(j)
 
-        steps = [(block, j) for block in rope_blocks for j in range(RUN)]
+        wide_steps = [(block, j) for block in rope_blocks[:3] for j in range(RUN)]
+        last = rope_blocks[3]
+        narrow_steps = [
+            (pair, first_j)
+            for pair in range(TILE_HEADS // PAIR_HEADS)
+            for first_j in range(0, RUN, PAIR_RUN)
+        ]
         jobs = []
-        to_reduce = []
         to_fold = []
-        for n, (block, j) in enumerate(steps):
-            acc = project(j, block)
-            direct, cross = rope_products(acc, j)
-            if to_reduce:
-                job_block, job_part, turned = to_reduce[0]
-                to_reduce = to_reduce[1:]
-                to_fold.append((job_block, job_part, reduce_slots(turned)))
-            rope_sum(block, j, direct, cross)
-            done = []
-            if n < RUN:
-                plain_bank(j, plain_blocks[0])
+        for n in range(len(wide_steps) + len(narrow_steps)):
+            if n < len(wide_steps):
+                block, j = wide_steps[n]
+                acc = project(j, block)
+                direct, cross = rope_products(acc, j, n == 0)
+                rope_sum(block, j, direct, cross)
+                if n + AHEAD < RUN:
+                    prepare_x(n + AHEAD)
                 if j == RUN - 1:
-                    done.append(plain_blocks[0])
-                if j + AHEAD < RUN:
-                    prepare_x(j + AHEAD)
-            elif n < 3 * RUN and n % 2 == 0:
-                plain_bank((n - RUN) // 2, plain_blocks[1])
-                if (n - RUN) // 2 == RUN - 1:
-                    done.append(plain_blocks[1])
-            if j == RUN - 1:
-                done.append(block)
-            for finished in done:
-                store_rows(finished)
-                for part in range(TILE_HEADS // TURN_HEADS):
-                    jobs.append((finished, part, n + 2))
-            if n % 2 == 1:
+                    store_rows(block, range(TILE_HEADS))
+                    for part in range(PARTS):
+                        jobs.append((block, part, n + 2))
+            else:
+                pair, first_j = narrow_steps[n - len(wide_steps)]
+                acc = project_pair(first_j, last, pair)
+                direct, cross = rope_products_pair(acc, first_j)
+                rope_sum_pair(last, pair, first_j, direct, cross)
+                if first_j + PAIR_RUN == RUN:
+                    store_rows(last, range(pair * PAIR_HEADS, (pair + 1) * PAIR_HEADS))
+                    if (pair + 1) * PAIR_HEADS % TURN_HEADS == 0:
+                        jobs.append((last, (pair + 1) * PAIR_HEADS // TURN_HEADS - 1, n + 2))
+            m = n - PLAIN_LAG
+            if 0 <= m < len(plain_blocks) * RUN:
+                plain_bank(m % RUN, plain_blocks[m // RUN])
+                if m % RUN == RUN - 1:
+                    store_rows(plain_blocks[m // RUN], range(TILE_HEADS))
+                    for part in range(PARTS):
+                        jobs.append((plain_blocks[m // RUN], part, n + 2))
+            if n >= FIRST_TURN and (n - FIRST_TURN) % 2 == 0:
                 if to_fold:
                     fold_and_store(*to_fold[0])
                     to_fold = to_fold[1:]
                 if jobs and jobs[0][2] <= n:
                     job_block, job_part, ready = jobs[0]
                     jobs = jobs[1:]
-                    to_reduce.append((job_block, job_part, turn_sums(job_block, job_part)))
+                    turned = turn_sums(job_block, job_part)
+                    to_fold.append((job_block, job_part, reduce_slots(turned)))
 
         for job_block, job_part, ready in jobs:
-            to_reduce.append((job_block, job_part, turn_sums(job_block, job_part)))
-            if len(to_reduce) > 1:
-                first_block, first_part, turned = to_reduce[0]
-                to_reduce = to_reduce[1:]
-                to_fold.append((first_block, first_part, reduce_slots(turned)))
-            if to_fold:
-                fold_and_store(*to_fold[0])
-                to_fold = to_fold[1:]
-        for job_block, job_part, turned in to_reduce:
+            turned = turn_sums(job_block, job_part)
             to_fold.append((job_block, job_part, reduce_slots(turned)))
         for waiting in to_fold:
             fold_and_store(*waiting)

@@ -131,26 +131,30 @@ def tile_causalselfattention2_pa_kernel(
                 out=sin_signed[:, :, :, 1].rearrange("p j i -> p (j i)"), in_=sin_bf[:]
             )
 
-        def prepare_x(j):
-            words = x_sb[:, j, :].bitcast(F32)
-            xt = bank_pool.tile([P, PASSES, 2, P], F32, tag="bank")
-            for g in range(PASSES):
-                for u in range(2):
-                    nc.tensor.transpose(
-                        xt[:, g, u, :],
-                        words[:, 2 * P * g + u : 2 * P * (g + 1) : 2],
-                        ident[:],
-                    )
-            grouped = stage.tile([P, PASSES * P * 4], BF16, align_bytes=64)
-            nc.scalar.copy(
-                out=grouped[:].bitcast(F32).rearrange("p (g r u) -> p g r u", g=PASSES, u=2),
-                in_=xt[:].rearrange("p g u r -> p g r u"),
-            )
-            nc.vector.quantize_mx(
-                out=x_codes[:, j, :].bitcast(FP8X4),
-                scales=x_scales[:, j, :],
-                in_=grouped[:],
-            )
+        def prepare_x(tiles):
+            turned_x = []
+            for j in tiles:
+                words = x_sb[:, j, :].bitcast(F32)
+                xt = bank_pool.tile([P, PASSES, 2, P], F32, tag="bank")
+                for g in range(PASSES):
+                    for u in range(2):
+                        nc.tensor.transpose(
+                            xt[:, g, u, :],
+                            words[:, 2 * P * g + u : 2 * P * (g + 1) : 2],
+                            ident[:],
+                        )
+                turned_x.append(xt)
+            for j, xt in zip(tiles, turned_x):
+                grouped = stage.tile([P, PASSES * P * 4], BF16, align_bytes=64)
+                nc.scalar.copy(
+                    out=grouped[:].bitcast(F32).rearrange("p (g r u) -> p g r u", g=PASSES, u=2),
+                    in_=xt[:].rearrange("p g u r -> p g r u"),
+                )
+                nc.vector.quantize_mx(
+                    out=x_codes[:, j, :].bitcast(FP8X4),
+                    scales=x_scales[:, j, :],
+                    in_=grouped[:],
+                )
 
         def project(j, block):
             first = block[0] * CHANNELS + block[1] * N_TILE
@@ -288,33 +292,37 @@ def tile_causalselfattention2_pa_kernel(
             )
             return sums
 
-        def fold_and_store(block, part, sums):
-            mean_ps = mean_pool.tile([P, HEAD], F32)
-            nc.tensor.matmul(
-                out=mean_ps[:],
-                lhsT=sums[:].rearrange("p q b -> p (q b)"),
-                rhs=fold[:],
-                start=True,
-                stop=True,
+        def fold_and_store(waiting):
+            mean_ps = mean_pool.tile([P, TILE_HEADS // TURN_HEADS, HEAD], F32)
+            for k, (block, part, sums) in enumerate(waiting):
+                nc.tensor.matmul(
+                    out=mean_ps[:, k, :],
+                    lhsT=sums[:].rearrange("p q b -> p (q b)"),
+                    rhs=fold[:],
+                    start=True,
+                    stop=True,
+                )
+            block, part, sums = waiting[0]
+            place = 4 * block[0] + 2 * block[1] + part
+            nc.scalar.copy(
+                out=means[:, place : place + len(waiting), :], in_=mean_ps[:, 0 : len(waiting), :]
             )
-            mean_sb = means[:, 4 * block[0] + 2 * block[1] + part, :]
-            nc.scalar.copy(out=mean_sb, in_=mean_ps[:])
-            first = (block[1] * TILE_HEADS + part * TURN_HEADS) * GROUPS
-            nc.sync.dma_start(
-                out=outs[block[0]]
-                .rearrange("b h g r d -> b (h g) r d")[
-                    :, first : first + TURN_HEADS * GROUPS, GROUP, :
-                ]
-                .rearrange("b q d -> q b d"),
-                in_=mean_sb,
-            )
+            for k, (block, part, sums) in enumerate(waiting):
+                first = (block[1] * TILE_HEADS + part * TURN_HEADS) * GROUPS
+                nc.sync.dma_start(
+                    out=outs[block[0]]
+                    .rearrange("b h g r d -> b (h g) r d")[
+                        :, first : first + TURN_HEADS * GROUPS, GROUP, :
+                    ]
+                    .rearrange("b q d -> q b d"),
+                    in_=means[:, place + k, :],
+                )
 
         AHEAD = 2
         PLAIN_LAG = 2
-        FIRST_TURN = RUN + 1
+        FIRST_TURN = RUN + 3
         PARTS = TILE_HEADS // TURN_HEADS
-        for j in range(AHEAD):
-            prepare_x(j)
+        prepare_x(range(AHEAD))
 
         wide_steps = [(block, j) for block in rope_blocks[:3] for j in range(RUN)]
         last = rope_blocks[3]
@@ -331,8 +339,8 @@ def tile_causalselfattention2_pa_kernel(
                 acc = project(j, block)
                 direct, cross = rope_products(acc, j, n == 0)
                 rope_sum(block, j, direct, cross)
-                if n + AHEAD < RUN:
-                    prepare_x(n + AHEAD)
+                if n % AHEAD == 0 and n + AHEAD < RUN:
+                    prepare_x(range(n + AHEAD, n + 2 * AHEAD))
                 if j == RUN - 1:
                     store_rows(block, range(TILE_HEADS))
                     for part in range(PARTS):
@@ -353,18 +361,17 @@ def tile_causalselfattention2_pa_kernel(
                     store_rows(plain_blocks[m // RUN], range(TILE_HEADS))
                     for part in range(PARTS):
                         jobs.append((plain_blocks[m // RUN], part, n + 2))
-            if n >= FIRST_TURN and (n - FIRST_TURN) % 2 == 0:
+            if n >= FIRST_TURN and (n - FIRST_TURN) % 4 == 0:
                 if to_fold:
-                    fold_and_store(*to_fold[0])
-                    to_fold = to_fold[1:]
-                if jobs and jobs[0][2] <= n:
-                    job_block, job_part, ready = jobs[0]
-                    jobs = jobs[1:]
-                    turned = turn_sums(job_block, job_part)
-                    to_fold.append((job_block, job_part, reduce_slots(turned)))
+                    fold_and_store(to_fold)
+                to_fold = []
+                ripe = [job for job in jobs[:2] if job[2] <= n]
+                jobs = jobs[len(ripe) :]
+                banks = [turn_sums(job[0], job[1]) for job in ripe]
+                for job, turned in zip(ripe, banks):
+                    to_fold.append((job[0], job[1], reduce_slots(turned)))
 
         for job_block, job_part, ready in jobs:
             turned = turn_sums(job_block, job_part)
             to_fold.append((job_block, job_part, reduce_slots(turned)))
-        for waiting in to_fold:
-            fold_and_store(*waiting)
+        fold_and_store(to_fold)

@@ -54,6 +54,7 @@ def tile_causalselfattention2_pa_kernel(
         ctx.enter_context(tc.manual_schedule())
 
         x_sb = keep.tile([P, RUN, CHANNELS], BF16)
+        x_sorted = keep.tile([P, RUN, CHANNELS // 2], F32)
         x_codes = keep.tile([P, RUN, PASSES * P], U32, align_bytes=64)
         x_scales = keep.tile([P, RUN, PASSES * P], U8, align_bytes=64)
         w_planes = keep.tile([P, PASSES, 3 * CHANNELS], U8, align_bytes=64)
@@ -113,9 +114,9 @@ def tile_causalselfattention2_pa_kernel(
         warm = keep.tile([P, 2], F32)
         nc.vector.memset(warm[:, 0:1], 0.0)
         nc.scalar.copy(out=warm[:, 1:2], in_=warm[:, 0:1])
-        fold = keep.tile([P, HEAD], F32)
-        nc.vector.tensor_tensor(out=fold[:], in0=ident[:, 0:HEAD], in1=ident[:, HEAD:P], op=ADD)
-        nc.vector.tensor_scalar_mul(out=fold[:], in0=fold[:], scalar1=1.0 / GROUP)
+        swap = keep.tile([P, P], F32)
+        nc.vector.tensor_copy(out=swap[:, 0:HEAD], in_=ident[:, HEAD:P])
+        nc.vector.tensor_copy(out=swap[:, HEAD:P], in_=ident[:, 0:HEAD])
         cos_dup = keep.tile([P, RUN, HEAD], F32)
         nc.vector.tensor_copy(
             out=cos_dup[:].rearrange("p j (i e) -> p (j i) e", e=2),
@@ -131,18 +132,25 @@ def tile_causalselfattention2_pa_kernel(
                 out=sin_signed[:, :, :, 1].rearrange("p j i -> p (j i)"), in_=sin_bf[:]
             )
 
-        def prepare_x(tiles):
+        def sort_x(tiles):
+            for j in tiles:
+                nc.scalar.copy(
+                    out=x_sorted[:, j, :].rearrange("p (g u r) -> p g u r", g=PASSES, u=2),
+                    in_=x_sb[:, j, :].bitcast(F32).rearrange("p (g r u) -> p g u r", g=PASSES, u=2),
+                )
+
+        def prepare_x(tiles, is_sorted):
             turned_x = []
             for j in tiles:
                 words = x_sb[:, j, :].bitcast(F32)
                 xt = bank_pool.tile([P, PASSES, 2, P], F32, tag="bank")
                 for g in range(PASSES):
                     for u in range(2):
-                        nc.tensor.transpose(
-                            xt[:, g, u, :],
-                            words[:, 2 * P * g + u : 2 * P * (g + 1) : 2],
-                            ident[:],
-                        )
+                        if is_sorted:
+                            some = x_sorted[:, j, (2 * g + u) * P : (2 * g + u + 1) * P]
+                        else:
+                            some = words[:, 2 * P * g + u : 2 * P * (g + 1) : 2]
+                        nc.tensor.transpose(xt[:, g, u, :], some, ident[:])
                 turned_x.append(xt)
             for j, xt in zip(tiles, turned_x):
                 grouped = stage.tile([P, PASSES * P * 4], BF16, align_bytes=64)
@@ -293,19 +301,23 @@ def tile_causalselfattention2_pa_kernel(
             return sums
 
         def fold_and_store(waiting):
-            mean_ps = mean_pool.tile([P, TILE_HEADS // TURN_HEADS, HEAD], F32)
+            mean_ps = mean_pool.tile([P, TILE_HEADS // TURN_HEADS, P], F32)
             for k, (block, part, sums) in enumerate(waiting):
-                nc.tensor.matmul(
-                    out=mean_ps[:, k, :],
-                    lhsT=sums[:].rearrange("p q b -> p (q b)"),
-                    rhs=fold[:],
-                    start=True,
-                    stop=True,
-                )
+                for turn, order in enumerate((ident, swap)):
+                    nc.tensor.matmul(
+                        out=mean_ps[:, k, :],
+                        lhsT=sums[:].rearrange("p q b -> p (q b)"),
+                        rhs=order[:],
+                        is_transpose=True,
+                        start=(turn == 0),
+                        stop=(turn == 1),
+                    )
             block, part, sums = waiting[0]
             place = 4 * block[0] + 2 * block[1] + part
-            nc.scalar.copy(
-                out=means[:, place : place + len(waiting), :], in_=mean_ps[:, 0 : len(waiting), :]
+            nc.scalar.mul(
+                out=means[:, place : place + len(waiting), :],
+                in_=mean_ps[:, 0 : len(waiting), 0:HEAD],
+                mul=1.0 / GROUP,
             )
             for k, (block, part, sums) in enumerate(waiting):
                 first = (block[1] * TILE_HEADS + part * TURN_HEADS) * GROUPS
@@ -322,7 +334,8 @@ def tile_causalselfattention2_pa_kernel(
         PLAIN_LAG = 2
         FIRST_TURN = RUN + 3
         PARTS = TILE_HEADS // TURN_HEADS
-        prepare_x(range(AHEAD))
+        prepare_x(range(AHEAD), False)
+        sort_x(range(AHEAD, 2 * AHEAD))
 
         wide_steps = [(block, j) for block in rope_blocks[:3] for j in range(RUN)]
         last = rope_blocks[3]
@@ -340,7 +353,8 @@ def tile_causalselfattention2_pa_kernel(
                 direct, cross = rope_products(acc, j, n == 0)
                 rope_sum(block, j, direct, cross)
                 if n % AHEAD == 0 and n + AHEAD < RUN:
-                    prepare_x(range(n + AHEAD, n + 2 * AHEAD))
+                    prepare_x(range(n + AHEAD, n + 2 * AHEAD), True)
+                    sort_x(range(n + 2 * AHEAD, min(n + 3 * AHEAD, RUN)))
                 if j == RUN - 1:
                     store_rows(block, range(TILE_HEADS))
                     for part in range(PARTS):

@@ -40,7 +40,7 @@ def tile_causalselfattention2_pa_kernel(
 ):
     nc = tc.nc
     outs = (out_0, out_1, out_2)
-    rope_blocks = [(K, 0), (Q, 0), (K, 1), (Q, 1)]
+    rope_blocks = [(K, 1), (Q, 0), (K, 0), (Q, 1)]
     plain_blocks = [(V, 0), (V, 1)]
 
     with ExitStack() as ctx:
@@ -54,10 +54,11 @@ def tile_causalselfattention2_pa_kernel(
         ctx.enter_context(tc.manual_schedule())
 
         x_sb = keep.tile([P, RUN, CHANNELS], BF16)
-        x_sorted = keep.tile([P, RUN, CHANNELS // 2], F32)
         x_codes = keep.tile([P, RUN, PASSES * P], U32, align_bytes=64)
         x_scales = keep.tile([P, RUN, PASSES * P], U8, align_bytes=64)
         w_planes = keep.tile([P, PASSES, 3 * CHANNELS], U8, align_bytes=64)
+        early_planes = keep.tile([P, PASSES, 2 * N_TILE], U8, align_bytes=64)
+        early_first = rope_blocks[0][0] * CHANNELS + rope_blocks[0][1] * N_TILE
         cos_bf = keep.tile([P, RUN * PAIRS], BF16)
         sin_bf = keep.tile([P, RUN * PAIRS], BF16)
         means = keep.tile([P, 3 * HEADS // TURN_HEADS, HEAD], F32)
@@ -69,7 +70,23 @@ def tile_causalselfattention2_pa_kernel(
                 [P, PASSES, N_TILE * WORD_BYTES], U8, name="w_words_%d_%d" % block, align_bytes=64
             )
 
+        nc.vector.memset(early_planes[:].rearrange("p g n -> p (g n)").bitcast(I32), 0)
         nc.vector.memset(w_planes[:].rearrange("p g n -> p (g n)").bitcast(I32), 0)
+
+        def load_planes(planes, first, width):
+            for r in range(4):
+                nc.sync.dma_start(
+                    out=planes[r:P:32, :, :].bitcast(I32),
+                    in_=w_attn_scales[:, r:16:4, first : first + width]
+                    .rearrange("g q n -> q g n")
+                    .bitcast(I32),
+                )
+
+        def planes_of(block, g, first, width):
+            column = block[0] * CHANNELS + block[1] * N_TILE + first
+            if block in (rope_blocks[0], plain_blocks[0]):
+                return early_planes[:, g, column - early_first : column - early_first + width]
+            return w_planes[:, g, column : column + width]
         x_tiles = x.rearrange("b (q j) k -> q b j k", j=RUN)
 
         def load_x(j):
@@ -96,11 +113,7 @@ def tile_causalselfattention2_pa_kernel(
         load_x(0)
         load_x(1)
         load_w_block(rope_blocks[0])
-        for r in range(4):
-            nc.sync.dma_start(
-                out=w_planes[r:P:32, :, :].bitcast(I32),
-                in_=w_attn_scales[:, r:16:4, :].rearrange("g q n -> q g n").bitcast(I32),
-            )
+        load_planes(early_planes, early_first, 2 * N_TILE)
         load_table(nc.scalar, cos_bf, freqs_cos)
         load_table(nc.sync, sin_bf, freqs_sin)
         load_x(2)
@@ -108,6 +121,7 @@ def tile_causalselfattention2_pa_kernel(
         load_w_block(plain_blocks[0])
         for j in range(4, RUN):
             load_x(j)
+        load_planes(w_planes, 0, 3 * CHANNELS)
         for block in (rope_blocks[1], plain_blocks[1], rope_blocks[2], rope_blocks[3]):
             load_w_block(block)
 
@@ -118,39 +132,35 @@ def tile_causalselfattention2_pa_kernel(
         nc.vector.tensor_copy(out=swap[:, 0:HEAD], in_=ident[:, HEAD:P])
         nc.vector.tensor_copy(out=swap[:, HEAD:P], in_=ident[:, 0:HEAD])
         cos_dup = keep.tile([P, RUN, HEAD], F32)
-        nc.vector.tensor_copy(
-            out=cos_dup[:].rearrange("p j (i e) -> p (j i) e", e=2),
-            in_=cos_bf[:].unsqueeze(2).to_broadcast([P, RUN * PAIRS, 2]),
-        )
+
+        def widen_cos():
+            nc.scalar.copy(
+                out=cos_dup[:].rearrange("p j (i e) -> p (j i) e", e=2),
+                in_=cos_bf[:].unsqueeze(2).to_broadcast([P, RUN * PAIRS, 2]),
+            )
+
         sin_signed = keep.tile([P, RUN, PAIRS, 2], F32)
 
         def widen_sin():
-            nc.vector.tensor_scalar_mul(
-                out=sin_signed[:, :, :, 0].rearrange("p j i -> p (j i)"), in0=sin_bf[:], scalar1=-1.0
+            nc.scalar.mul(
+                out=sin_signed[:, :, :, 0].rearrange("p j i -> p (j i)"), in_=sin_bf[:], mul=-1.0
             )
-            nc.vector.tensor_copy(
+            nc.scalar.copy(
                 out=sin_signed[:, :, :, 1].rearrange("p j i -> p (j i)"), in_=sin_bf[:]
             )
 
-        def sort_x(tiles):
-            for j in tiles:
-                nc.scalar.copy(
-                    out=x_sorted[:, j, :].rearrange("p (g u r) -> p g u r", g=PASSES, u=2),
-                    in_=x_sb[:, j, :].bitcast(F32).rearrange("p (g r u) -> p g u r", g=PASSES, u=2),
-                )
-
-        def prepare_x(tiles, is_sorted):
+        def prepare_x(tiles):
             turned_x = []
             for j in tiles:
                 words = x_sb[:, j, :].bitcast(F32)
                 xt = bank_pool.tile([P, PASSES, 2, P], F32, tag="bank")
                 for g in range(PASSES):
                     for u in range(2):
-                        if is_sorted:
-                            some = x_sorted[:, j, (2 * g + u) * P : (2 * g + u + 1) * P]
-                        else:
-                            some = words[:, 2 * P * g + u : 2 * P * (g + 1) : 2]
-                        nc.tensor.transpose(xt[:, g, u, :], some, ident[:])
+                        nc.tensor.transpose(
+                            xt[:, g, u, :],
+                            words[:, 2 * P * g + u : 2 * P * (g + 1) : 2],
+                            ident[:],
+                        )
                 turned_x.append(xt)
             for j, xt in zip(tiles, turned_x):
                 grouped = stage.tile([P, PASSES * P * 4], BF16, align_bytes=64)
@@ -164,6 +174,30 @@ def tile_causalselfattention2_pa_kernel(
                     in_=grouped[:],
                 )
 
+        def prepare_first_x():
+            words = x_sb[:, 0, :].bitcast(F32)
+            halves = []
+            for g in range(PASSES):
+                xt = bank_pool.tile([P, 2, P], F32, tag="bank")
+                for u in range(2):
+                    nc.tensor.transpose(
+                        xt[:, u, :], words[:, 2 * P * g + u : 2 * P * (g + 1) : 2], ident[:]
+                    )
+                halves.append(xt)
+            grouped = stage.tile([P, PASSES * P * 4], BF16, align_bytes=64)
+            for g in range(PASSES):
+                nc.scalar.copy(
+                    out=grouped[:, g * P * 4 : (g + 1) * P * 4]
+                    .bitcast(F32)
+                    .rearrange("p (r u) -> p r u", u=2),
+                    in_=halves[g][:].rearrange("p u r -> p r u"),
+                )
+                nc.vector.quantize_mx(
+                    out=x_codes[:, 0, g * P : (g + 1) * P].bitcast(FP8X4),
+                    scales=x_scales[:, 0, g * P : (g + 1) * P],
+                    in_=grouped[:, g * P * 4 : (g + 1) * P * 4],
+                )
+
         def project(j, block):
             first = block[0] * CHANNELS + block[1] * N_TILE
             acc = bank_pool.tile([P, N_TILE], F32, tag="bank")
@@ -174,7 +208,7 @@ def tile_causalselfattention2_pa_kernel(
                     lhsT=x_codes[:, j, tokens].bitcast(FP8X4),
                     lhsT_scale=x_scales[:, j, tokens],
                     rhs=w_words[block][:, g, :].bitcast(FP4X4),
-                    rhs_scale=w_planes[:, g, first : first + N_TILE],
+                    rhs_scale=planes_of(block, g, 0, N_TILE),
                     start=(g == 0),
                     stop=(g == PASSES - 1),
                 )
@@ -193,7 +227,7 @@ def tile_causalselfattention2_pa_kernel(
                         rhs=w_words[block][
                             :, g, pair * N_PAIR * WORD_BYTES : (pair + 1) * N_PAIR * WORD_BYTES
                         ].bitcast(FP4X4),
-                        rhs_scale=w_planes[:, g, first : first + N_PAIR],
+                        rhs_scale=planes_of(block, g, pair * N_PAIR, N_PAIR),
                         start=(g == 0),
                         stop=(g == PASSES - 1),
                     )
@@ -220,8 +254,8 @@ def tile_causalselfattention2_pa_kernel(
             )
             return direct, cross
 
-        def rope_sum_pair(block, pair, first_j, direct, cross):
-            nc.gpsimd.tensor_tensor(
+        def rope_sum_pair(engine, block, pair, first_j, direct, cross):
+            engine.tensor_tensor(
                 out=rows[block][
                     :, pair * PAIR_HEADS : (pair + 1) * PAIR_HEADS, first_j : first_j + PAIR_RUN, :
                 ].rearrange("p h j d -> p j h d"),
@@ -230,7 +264,7 @@ def tile_causalselfattention2_pa_kernel(
                 op=ADD,
             )
 
-        def rope_products(acc, j, first):
+        def rope_products(acc, j):
             direct = prod.tile([P, TILE_HEADS, HEAD], F32, tag="direct")
             nc.vector.tensor_tensor(
                 out=direct[:],
@@ -238,8 +272,6 @@ def tile_causalselfattention2_pa_kernel(
                 in1=cos_dup[:, j, :].unsqueeze(1).to_broadcast([P, TILE_HEADS, HEAD]),
                 op=MULT,
             )
-            if first:
-                widen_sin()
             pairs = acc[:].rearrange("p (h i e) -> p h i e", i=PAIRS, e=2)
             cross = prod.tile([P, TILE_HEADS, PAIRS, 2], F32, tag="cross")
             nc.vector.tensor_tensor(
@@ -290,14 +322,18 @@ def tile_causalselfattention2_pa_kernel(
                     )
             return turned
 
-        def reduce_slots(turned):
+        def reduce_slots(turned, pieces):
             sums = small.tile([P, TURN_HEADS * GROUPS, BATCH], F32)
-            nc.vector.tensor_reduce(
-                out=sums[:],
-                in_=turned[:].rearrange("p h (g s b) -> p (h g) b s", s=SLOTS, b=BATCH),
-                axis=mybir.AxisListType.X,
-                op=ADD,
-            )
+            heads = TURN_HEADS // pieces
+            for piece in range(pieces):
+                nc.vector.tensor_reduce(
+                    out=sums[:, piece * heads * GROUPS : (piece + 1) * heads * GROUPS, :],
+                    in_=turned[:, piece * heads : (piece + 1) * heads, :].rearrange(
+                        "p h (g s b) -> p (h g) b s", s=SLOTS, b=BATCH
+                    ),
+                    axis=mybir.AxisListType.X,
+                    op=ADD,
+                )
             return sums
 
         def fold_and_store(waiting):
@@ -334,8 +370,10 @@ def tile_causalselfattention2_pa_kernel(
         PLAIN_LAG = 2
         FIRST_TURN = RUN + 3
         PARTS = TILE_HEADS // TURN_HEADS
-        prepare_x(range(AHEAD), False)
-        sort_x(range(AHEAD, 2 * AHEAD))
+        prepare_first_x()
+        widen_cos()
+        prepare_x(range(1, AHEAD))
+        widen_sin()
 
         wide_steps = [(block, j) for block in rope_blocks[:3] for j in range(RUN)]
         last = rope_blocks[3]
@@ -350,11 +388,10 @@ def tile_causalselfattention2_pa_kernel(
             if n < len(wide_steps):
                 block, j = wide_steps[n]
                 acc = project(j, block)
-                direct, cross = rope_products(acc, j, n == 0)
+                direct, cross = rope_products(acc, j)
                 rope_sum(block, j, direct, cross)
                 if n % AHEAD == 0 and n + AHEAD < RUN:
-                    prepare_x(range(n + AHEAD, n + 2 * AHEAD), True)
-                    sort_x(range(n + 2 * AHEAD, min(n + 3 * AHEAD, RUN)))
+                    prepare_x(range(n + AHEAD, n + 2 * AHEAD))
                 if j == RUN - 1:
                     store_rows(block, range(TILE_HEADS))
                     for part in range(PARTS):
@@ -363,7 +400,10 @@ def tile_causalselfattention2_pa_kernel(
                 pair, first_j = narrow_steps[n - len(wide_steps)]
                 acc = project_pair(first_j, last, pair)
                 direct, cross = rope_products_pair(acc, first_j)
-                rope_sum_pair(last, pair, first_j, direct, cross)
+                is_last = n == len(wide_steps) + len(narrow_steps) - 1
+                rope_sum_pair(
+                    nc.vector if is_last else nc.gpsimd, last, pair, first_j, direct, cross
+                )
                 if first_j + PAIR_RUN == RUN:
                     store_rows(last, range(pair * PAIR_HEADS, (pair + 1) * PAIR_HEADS))
                     if (pair + 1) * PAIR_HEADS % TURN_HEADS == 0:
@@ -383,9 +423,9 @@ def tile_causalselfattention2_pa_kernel(
                 jobs = jobs[len(ripe) :]
                 banks = [turn_sums(job[0], job[1]) for job in ripe]
                 for job, turned in zip(ripe, banks):
-                    to_fold.append((job[0], job[1], reduce_slots(turned)))
+                    to_fold.append((job[0], job[1], reduce_slots(turned, 1)))
 
         for job_block, job_part, ready in jobs:
             turned = turn_sums(job_block, job_part)
-            to_fold.append((job_block, job_part, reduce_slots(turned)))
+            to_fold.append((job_block, job_part, reduce_slots(turned, TURN_HEADS // PAIR_HEADS)))
         fold_and_store(to_fold)

@@ -296,14 +296,16 @@ def tile_causalselfattention2_pa_kernel(
                 out=rows[block][:, :, j, :], in_=acc[:].rearrange("p (h d) -> p h d", d=HEAD)
             )
 
-        def store_rows(block, heads):
+        def store_rows(block, heads, first_j=0, count=RUN):
             for h in heads:
                 for b in range(BATCH):
                     nc.sync.dma_start(
-                        out=outs[block[0]][
-                            b, block[1] * TILE_HEADS + h, :, 0:GROUP, :
-                        ].rearrange("g (s j) d -> g s (j d)", j=RUN),
-                        in_=rows[block][b:P:2, h, :, :].rearrange("p j d -> p (j d)"),
+                        out=outs[block[0]][b, block[1] * TILE_HEADS + h, :, 0:GROUP, :].rearrange(
+                            "g (s j) d -> g s j d", j=RUN
+                        )[:, :, first_j : first_j + count, :].rearrange("g s j d -> g s (j d)"),
+                        in_=rows[block][b:P:2, h, first_j : first_j + count, :].rearrange(
+                            "p j d -> p (j d)"
+                        ),
                     )
 
         def turn_sums(block, part):
@@ -392,8 +394,11 @@ def tile_causalselfattention2_pa_kernel(
                 rope_sum(block, j, direct, cross)
                 if n % AHEAD == 0 and n + AHEAD < RUN:
                     prepare_x(range(n + AHEAD, n + 2 * AHEAD))
-                if j == RUN - 1:
+                if block == rope_blocks[0] and j % (RUN // 2) == RUN // 2 - 1:
+                    store_rows(block, range(TILE_HEADS), j + 1 - RUN // 2, RUN // 2)
+                elif j == RUN - 1:
                     store_rows(block, range(TILE_HEADS))
+                if j == RUN - 1:
                     for part in range(PARTS):
                         jobs.append((block, part, n + 2))
             else:
@@ -411,8 +416,11 @@ def tile_causalselfattention2_pa_kernel(
             m = n - PLAIN_LAG
             if 0 <= m < len(plain_blocks) * RUN:
                 plain_bank(m % RUN, plain_blocks[m // RUN])
-                if m % RUN == RUN - 1:
+                if m // RUN == 0 and m % (RUN // 2) == RUN // 2 - 1:
+                    store_rows(plain_blocks[0], range(TILE_HEADS), m + 1 - RUN // 2, RUN // 2)
+                elif m % RUN == RUN - 1:
                     store_rows(plain_blocks[m // RUN], range(TILE_HEADS))
+                if m % RUN == RUN - 1:
                     for part in range(PARTS):
                         jobs.append((plain_blocks[m // RUN], part, n + 2))
             if n >= FIRST_TURN and (n - FIRST_TURN) % 4 == 0:

@@ -116,9 +116,9 @@ def tile_causalselfattention2_pa_kernel(
         load_planes(early_planes, early_first, 2 * N_TILE)
         load_table(nc.scalar, cos_bf, freqs_cos)
         load_table(nc.sync, sin_bf, freqs_sin)
+        load_w_block(plain_blocks[0])
         load_x(2)
         load_x(3)
-        load_w_block(plain_blocks[0])
         for j in range(4, RUN):
             load_x(j)
         load_planes(w_planes, 0, 3 * CHANNELS)
@@ -369,7 +369,7 @@ def tile_causalselfattention2_pa_kernel(
                 )
 
         AHEAD = 2
-        PLAIN_LAG = 2
+        PLAIN_LAG = 0
         FIRST_TURN = RUN + 3
         PARTS = TILE_HEADS // TURN_HEADS
         prepare_first_x()

from contextlib import ExitStack

import concourse.mybir as mybir
from concourse.masks import make_identity

F32 = mybir.dt.float32
BF16 = mybir.dt.bfloat16
I32 = mybir.dt.int32
U32 = mybir.dt.uint32
U8 = mybir.dt.uint8
FP8X4 = mybir.dt.float8_e4m3fn_x4
FP4X4 = mybir.dt.float4_e2m1fn_x4
MULT = mybir.AluOpType.mult
ADD = mybir.AluOpType.add

P = 128
BATCH, SEQ, CHANNELS = 2, 512, 1024
HEADS, HEAD = 16, 64
PAIRS = HEAD // 2
GROUPS, GROUP = 16, 32
K_PASS = 4 * P
PASSES = CHANNELS // K_PASS
RUN = 8
SLOTS = GROUP // RUN
RUNS = SEQ // RUN
N_TILE = 512
TILE_HEADS = N_TILE // HEAD
TURN_HEADS = 4
PAIR_HEADS = 2
N_PAIR = PAIR_HEADS * HEAD
PAIR_RUN = N_TILE // N_PAIR
WORD_BYTES = 2
Q, K, V = 0, 1, 2

FLOPS = 2 * BATCH * SEQ * CHANNELS * 3 * CHANNELS


def tile_causalselfattention2_pa_kernel(
    tc, x, w_attn_words, w_attn_scales, freqs_cos, freqs_sin, out_0, out_1, out_2
):
    nc = tc.nc
    outs = (out_0, out_1, out_2)
    rope_blocks = [(K, 1), (Q, 0), (K, 0), (Q, 1)]
    plain_blocks = [(V, 0), (V, 1)]

    with ExitStack() as ctx:
        keep = ctx.enter_context(tc.tile_pool(name="keep", bufs=1))
        stage = ctx.enter_context(tc.tile_pool(name="stage", bufs=3))
        prod = ctx.enter_context(tc.tile_pool(name="prod", bufs=4))
        small = ctx.enter_context(tc.tile_pool(name="small", bufs=2))
        bank_pool = ctx.enter_context(tc.psum_pool(name="bank", bufs=5))
        turned_pool = ctx.enter_context(tc.psum_pool(name="turned", bufs=2))
        mean_pool = ctx.enter_context(tc.psum_pool(name="mean", bufs=1))
        ctx.enter_context(tc.manual_schedule())

        x_sb = keep.tile([P, RUN, CHANNELS], BF16)
        x_codes = keep.tile([P, RUN, PASSES * P], U32, align_bytes=64)
        x_scales = keep.tile([P, RUN, PASSES * P], U8, align_bytes=64)
        w_planes = keep.tile([P, PASSES, 3 * CHANNELS], U8, align_bytes=64)
        early_planes = keep.tile([P, PASSES, 2 * N_TILE], U8, align_bytes=64)
        early_first = rope_blocks[0][0] * CHANNELS + rope_blocks[0][1] * N_TILE
        cos_bf = keep.tile([P, RUN * PAIRS], BF16)
        sin_bf = keep.tile([P, RUN * PAIRS], BF16)
        means = keep.tile([P, 3 * HEADS // TURN_HEADS, HEAD], F32)
        rows = {}
        w_words = {}
        for block in rope_blocks + plain_blocks:
            rows[block] = keep.tile([P, TILE_HEADS, RUN, HEAD], F32, name="rows_%d_%d" % block)
            w_words[block] = keep.tile(
                [P, PASSES, N_TILE * WORD_BYTES], U8, name="w_words_%d_%d" % block, align_bytes=64
            )

        nc.vector.memset(early_planes[:].rearrange("p g n -> p (g n)").bitcast(I32), 0)
        nc.vector.memset(w_planes[:].rearrange("p g n -> p (g n)").bitcast(I32), 0)

        def load_planes(planes, first, width):
            for r in range(4):
                nc.sync.dma_start(
                    out=planes[r:P:32, :, :].bitcast(I32),
                    in_=w_attn_scales[:, r:16:4, first : first + width]
                    .rearrange("g q n -> q g n")
                    .bitcast(I32),
                )

        def planes_of(block, g, first, width):
            column = block[0] * CHANNELS + block[1] * N_TILE + first
            if block in (rope_blocks[0], plain_blocks[0]):
                return early_planes[:, g, column - early_first : column - early_first + width]
            return w_planes[:, g, column : column + width]
        x_tiles = x.rearrange("b (q j) k -> q b j k", j=RUN)

        def load_x(j):
            nc.sync.dma_start(out=x_sb[:, j, :], in_=x_tiles[:, :, j, :])

        def load_w_block(block):
            first = (block[0] * CHANNELS + block[1] * N_TILE) * WORD_BYTES
            cols = slice(first, first + N_TILE * WORD_BYTES)
            nc.sync.dma_start(
                out=w_words[block][:].bitcast(I32),
                in_=w_attn_words[:, :, cols].rearrange("g p c -> p g c").bitcast(I32),
            )

        def load_table(queue, table_bf, table):
            queue.dma_start(
                out=table_bf[:],
                in_=table.rearrange("(q j) i -> q (j i)", j=RUN)
                .unsqueeze(1)
                .to_broadcast([RUNS, BATCH, RUN * PAIRS]),
            )

        ident = keep.tile([P, P], F32)
        make_identity(nc, ident[:])
        load_x(0)
        load_x(1)
        load_w_block(rope_blocks[0])
        load_planes(early_planes, early_first, 2 * N_TILE)
        load_table(nc.scalar, cos_bf, freqs_cos)
        load_table(nc.sync, sin_bf, freqs_sin)
        load_w_block(plain_blocks[0])
        load_x(2)
        load_x(3)
        for j in range(4, RUN):
            load_x(j)
        load_planes(w_planes, 0, 3 * CHANNELS)
        for block in (rope_blocks[1], plain_blocks[1], rope_blocks[2], rope_blocks[3]):
            load_w_block(block)

        warm = keep.tile([P, 2], F32)
        nc.vector.memset(warm[:, 0:1], 0.0)
        nc.scalar.copy(out=warm[:, 1:2], in_=warm[:, 0:1])
        swap = keep.tile([P, P], F32)
        nc.vector.tensor_copy(out=swap[:, 0:HEAD], in_=ident[:, HEAD:P])
        nc.vector.tensor_copy(out=swap[:, HEAD:P], in_=ident[:, 0:HEAD])
        cos_dup = keep.tile([P, RUN, HEAD], F32)

        def widen_cos():
            nc.scalar.copy(
                out=cos_dup[:].rearrange("p j (i e) -> p (j i) e", e=2),
                in_=cos_bf[:].unsqueeze(2).to_broadcast([P, RUN * PAIRS, 2]),
            )

        sin_signed = keep.tile([P, RUN, PAIRS, 2], F32)

        def widen_sin():
            nc.scalar.mul(
                out=sin_signed[:, :, :, 0].rearrange("p j i -> p (j i)"), in_=sin_bf[:], mul=-1.0
            )
            nc.scalar.copy(
                out=sin_signed[:, :, :, 1].rearrange("p j i -> p (j i)"), in_=sin_bf[:]
            )

        def prepare_x(tiles):
            turned_x = []
            for j in tiles:
                words = x_sb[:, j, :].bitcast(F32)
                xt = bank_pool.tile([P, PASSES, 2, P], F32, tag="bank")
                for g in range(PASSES):
                    for u in range(2):
                        nc.tensor.transpose(
                            xt[:, g, u, :],
                            words[:, 2 * P * g + u : 2 * P * (g + 1) : 2],
                            ident[:],
                        )
                turned_x.append(xt)
            for j, xt in zip(tiles, turned_x):
                grouped = stage.tile([P, PASSES * P * 4], BF16, align_bytes=64)
                nc.scalar.copy(
                    out=grouped[:].bitcast(F32).rearrange("p (g r u) -> p g r u", g=PASSES, u=2),
                    in_=xt[:].rearrange("p g u r -> p g r u"),
                )
                nc.vector.quantize_mx(
                    out=x_codes[:, j, :].bitcast(FP8X4),
                    scales=x_scales[:, j, :],
                    in_=grouped[:],
                )

        def prepare_first_x():
            words = x_sb[:, 0, :].bitcast(F32)
            halves = []
            for g in range(PASSES):
                xt = bank_pool.tile([P, 2, P], F32, tag="bank")
                for u in range(2):
                    nc.tensor.transpose(
                        xt[:, u, :], words[:, 2 * P * g + u : 2 * P * (g + 1) : 2], ident[:]
                    )
                halves.append(xt)
            grouped = stage.tile([P, PASSES * P * 4], BF16, align_bytes=64)
            for g in range(PASSES):
                nc.scalar.copy(
                    out=grouped[:, g * P * 4 : (g + 1) * P * 4]
                    .bitcast(F32)
                    .rearrange("p (r u) -> p r u", u=2),
                    in_=halves[g][:].rearrange("p u r -> p r u"),
                )
                nc.vector.quantize_mx(
                    out=x_codes[:, 0, g * P : (g + 1) * P].bitcast(FP8X4),
                    scales=x_scales[:, 0, g * P : (g + 1) * P],
                    in_=grouped[:, g * P * 4 : (g + 1) * P * 4],
                )

        def project(j, block):
            first = block[0] * CHANNELS + block[1] * N_TILE
            acc = bank_pool.tile([P, N_TILE], F32, tag="bank")
            for g in range(PASSES):
                tokens = slice(g * P, (g + 1) * P)
                nc.tensor.matmul_mx(
                    out=acc[:],
                    lhsT=x_codes[:, j, tokens].bitcast(FP8X4),
                    lhsT_scale=x_scales[:, j, tokens],
                    rhs=w_words[block][:, g, :].bitcast(FP4X4),
                    rhs_scale=planes_of(block, g, 0, N_TILE),
                    start=(g == 0),
                    stop=(g == PASSES - 1),
                )
            return acc

        def project_pair(first_j, block, pair):
            first = block[0] * CHANNELS + block[1] * N_TILE + pair * N_PAIR
            acc = bank_pool.tile([P, PAIR_RUN, N_PAIR], F32, tag="bank")
            for jj in range(PAIR_RUN):
                for g in range(PASSES):
                    tokens = slice(g * P, (g + 1) * P)
                    nc.tensor.matmul_mx(
                        out=acc[:, jj, :],
                        lhsT=x_codes[:, first_j + jj, tokens].bitcast(FP8X4),
                        lhsT_scale=x_scales[:, first_j + jj, tokens],
                        rhs=w_words[block][
                            :, g, pair * N_PAIR * WORD_BYTES : (pair + 1) * N_PAIR * WORD_BYTES
                        ].bitcast(FP4X4),
                        rhs_scale=planes_of(block, g, pair * N_PAIR, N_PAIR),
                        start=(g == 0),
                        stop=(g == PASSES - 1),
                    )
            return acc

        def rope_products_pair(acc, first_j):
            some = slice(first_j, first_j + PAIR_RUN)
            direct = prod.tile([P, PAIR_RUN, PAIR_HEADS, HEAD], F32, tag="direct")
            nc.vector.tensor_tensor(
                out=direct[:],
                in0=acc[:].rearrange("p j (h d) -> p j h d", d=HEAD),
                in1=cos_dup[:, some, :].unsqueeze(2).to_broadcast([P, PAIR_RUN, PAIR_HEADS, HEAD]),
                op=MULT,
            )
            pairs = acc[:].rearrange("p j (h i e) -> p j h i e", i=PAIRS, e=2)
            cross = prod.tile([P, PAIR_RUN, PAIR_HEADS, PAIRS, 2], F32, tag="cross")
            nc.vector.tensor_tensor(
                out=cross[:],
                in0=pairs[:, :, :, :, ::-1],
                in1=sin_signed[:, some, :, :]
                .unsqueeze(2)
                .to_broadcast([P, PAIR_RUN, PAIR_HEADS, PAIRS, 2]),
                op=MULT,
            )
            return direct, cross

        def rope_sum_pair(engine, block, pair, first_j, direct, cross):
            engine.tensor_tensor(
                out=rows[block][
                    :, pair * PAIR_HEADS : (pair + 1) * PAIR_HEADS, first_j : first_j + PAIR_RUN, :
                ].rearrange("p h j d -> p j h d"),
                in0=direct[:],
                in1=cross[:].rearrange("p j h i e -> p j h (i e)"),
                op=ADD,
            )

        def rope_products(acc, j):
            direct = prod.tile([P, TILE_HEADS, HEAD], F32, tag="direct")
            nc.vector.tensor_tensor(
                out=direct[:],
                in0=acc[:].rearrange("p (h d) -> p h d", d=HEAD),
                in1=cos_dup[:, j, :].unsqueeze(1).to_broadcast([P, TILE_HEADS, HEAD]),
                op=MULT,
            )
            pairs = acc[:].rearrange("p (h i e) -> p h i e", i=PAIRS, e=2)
            cross = prod.tile([P, TILE_HEADS, PAIRS, 2], F32, tag="cross")
            nc.vector.tensor_tensor(
                out=cross[:],
                in0=pairs[:, :, :, ::-1],
                in1=sin_signed[:, j, :, :].unsqueeze(1).to_broadcast([P, TILE_HEADS, PAIRS, 2]),
                op=MULT,
            )
            return direct, cross

        def rope_sum(block, j, direct, cross):
            nc.gpsimd.tensor_tensor(
                out=rows[block][:, :, j, :],
                in0=direct[:],
                in1=cross[:].rearrange("p h i e -> p h (i e)"),
                op=ADD,
            )

        def plain_bank(j, block):
            acc = project(j, block)
            nc.scalar.copy(
                out=rows[block][:, :, j, :], in_=acc[:].rearrange("p (h d) -> p h d", d=HEAD)
            )

        def store_rows(block, heads, first_j=0, count=RUN):
            for h in heads:
                for b in range(BATCH):
                    nc.sync.dma_start(
                        out=outs[block[0]][b, block[1] * TILE_HEADS + h, :, 0:GROUP, :].rearrange(
                            "g (s j) d -> g s j d", j=RUN
                        )[:, :, first_j : first_j + count, :].rearrange("g s j d -> g s (j d)"),
                        in_=rows[block][b:P:2, h, first_j : first_j + count, :].rearrange(
                            "p j d -> p (j d)"
                        ),
                    )

        def turn_sums(block, part):
            turned = turned_pool.tile([P, TURN_HEADS, P], F32)
            for hh in range(TURN_HEADS):
                for m in range(RUN // 2):
                    nc.tensor.matmul(
                        out=turned[:, hh, :],
                        lhsT=rows[block][
                            :, part * TURN_HEADS + hh, 2 * m : 2 * m + 2, :
                        ].rearrange("p j d -> p (j d)"),
                        rhs=ident[:],
                        is_transpose=True,
                        start=(m == 0),
                        stop=(m == RUN // 2 - 1),
                    )
            return turned

        def reduce_slots(turned, pieces):
            sums = small.tile([P, TURN_HEADS * GROUPS, BATCH], F32)
            heads = TURN_HEADS // pieces
            for piece in range(pieces):
                nc.vector.tensor_reduce(
                    out=sums[:, piece * heads * GROUPS : (piece + 1) * heads * GROUPS, :],
                    in_=turned[:, piece * heads : (piece + 1) * heads, :].rearrange(
                        "p h (g s b) -> p (h g) b s", s=SLOTS, b=BATCH
                    ),
                    axis=mybir.AxisListType.X,
                    op=ADD,
                )
            return sums

        def fold_and_store(waiting):
            mean_ps = mean_pool.tile([P, TILE_HEADS // TURN_HEADS, P], F32)
            for k, (block, part, sums) in enumerate(waiting):
                for turn, order in enumerate((ident, swap)):
                    nc.tensor.matmul(
                        out=mean_ps[:, k, :],
                        lhsT=sums[:].rearrange("p q b -> p (q b)"),
                        rhs=order[:],
                        is_transpose=True,
                        start=(turn == 0),
                        stop=(turn == 1),
                    )
            block, part, sums = waiting[0]
            place = 4 * block[0] + 2 * block[1] + part
            nc.scalar.mul(
                out=means[:, place : place + len(waiting), :],
                in_=mean_ps[:, 0 : len(waiting), 0:HEAD],
                mul=1.0 / GROUP,
            )
            for k, (block, part, sums) in enumerate(waiting):
                first = (block[1] * TILE_HEADS + part * TURN_HEADS) * GROUPS
                nc.sync.dma_start(
                    out=outs[block[0]]
                    .rearrange("b h g r d -> b (h g) r d")[
                        :, first : first + TURN_HEADS * GROUPS, GROUP, :
                    ]
                    .rearrange("b q d -> q b d"),
                    in_=means[:, place + k, :],
                )

        AHEAD = 2
        PLAIN_LAG = 0
        FIRST_TURN = RUN + 3
        PARTS = TILE_HEADS // TURN_HEADS
        prepare_first_x()
        widen_cos()
        prepare_x(range(1, AHEAD))
        widen_sin()

        wide_steps = [(block, j) for block in rope_blocks[:3] for j in range(RUN)]
        last = rope_blocks[3]
        narrow_steps = [
            (pair, first_j)
            for pair in range(TILE_HEADS // PAIR_HEADS)
            for first_j in range(0, RUN, PAIR_RUN)
        ]
        jobs = []
        to_fold = []
        for n in range(len(wide_steps) + len(narrow_steps)):
            if n < len(wide_steps):
                block, j = wide_steps[n]
                acc = project(j, block)
                direct, cross = rope_products(acc, j)
                rope_sum(block, j, direct, cross)
                if n % AHEAD == 0 and n + AHEAD < RUN:
                    prepare_x(range(n + AHEAD, n + 2 * AHEAD))
                if block == rope_blocks[0] and j % (RUN // 2) == RUN // 2 - 1:
                    store_rows(block, range(TILE_HEADS), j + 1 - RUN // 2, RUN // 2)
                elif j == RUN - 1:
                    store_rows(block, range(TILE_HEADS))
                if j == RUN - 1:
                    for part in range(PARTS):
                        jobs.append((block, part, n + 2))
            else:
                pair, first_j = narrow_steps[n - len(wide_steps)]
                acc = project_pair(first_j, last, pair)
                direct, cross = rope_products_pair(acc, first_j)
                is_last = n == len(wide_steps) + len(narrow_steps) - 1
                rope_sum_pair(
                    nc.vector if is_last else nc.gpsimd, last, pair, first_j, direct, cross
                )
                if first_j + PAIR_RUN == RUN:
                    store_rows(last, range(pair * PAIR_HEADS, (pair + 1) * PAIR_HEADS))
                    if (pair + 1) * PAIR_HEADS % TURN_HEADS == 0:
                        jobs.append((last, (pair + 1) * PAIR_HEADS // TURN_HEADS - 1, n + 2))
            m = n - PLAIN_LAG
            if 0 <= m < len(plain_blocks) * RUN:
                plain_bank(m % RUN, plain_blocks[m // RUN])
                if m // RUN == 0 and m % (RUN // 2) == RUN // 2 - 1:
                    store_rows(plain_blocks[0], range(TILE_HEADS), m + 1 - RUN // 2, RUN // 2)
                elif m % RUN == RUN - 1:
                    store_rows(plain_blocks[m // RUN], range(TILE_HEADS))
                if m % RUN == RUN - 1:
                    for part in range(PARTS):
                        jobs.append((plain_blocks[m // RUN], part, n + 2))
            if n >= FIRST_TURN and (n - FIRST_TURN) % 4 == 0:
                if to_fold:
                    fold_and_store(to_fold)
                to_fold = []
                ripe = [job for job in jobs[:2] if job[2] <= n]
                jobs = jobs[len(ripe) :]
                banks = [turn_sums(job[0], job[1]) for job in ripe]
                for job, turned in zip(ripe, banks):
                    to_fold.append((job[0], job[1], reduce_slots(turned, 1)))

        for job_block, job_part, ready in jobs:
            turned = turn_sums(job_block, job_part)
            to_fold.append((job_block, job_part, reduce_slots(turned, TURN_HEADS // PAIR_HEADS)))
        fold_and_store(to_fold)
